import numpy as np
import ml_dtypes


def mxq(x, axis, fmt="e4m3"):
    dtype, down = {"e4m3": (ml_dtypes.float8_e4m3fn, 7), "e5m2": (ml_dtypes.float8_e5m2, 14)}[fmt]
    v = np.moveaxis(np.asarray(x, np.float32).astype(ml_dtypes.bfloat16).astype(np.float64), axis, -1)
    blocks = v.reshape(v.shape[:-1] + (-1, 32))
    amax = np.abs(blocks).max(-1, keepdims=True)
    byte = np.maximum(np.where(amax > 0, np.frexp(amax)[1] - 1 + 127, 0) - down, 1)
    scale = np.exp2(byte - 127.0)
    codes = (blocks / scale).astype(np.float32).astype(dtype).astype(np.float64)
    return np.moveaxis((codes * scale).reshape(v.shape), -1, axis)


WIDE = False


def mx_kscale(k):
    if not WIDE:
        return np.ones(k)
    levels = np.array([10, -10, 5, -5, 0])
    a = np.random.permutation(np.resize(levels, k // 512 * 4)).reshape(k // 512, 4)
    idx = np.arange(k)
    return np.exp2(a[idx // 512, idx % 128 // 32])


BF16 = ml_dtypes.bfloat16


def bf(x):
    return np.asarray(x, np.float32).astype(BF16)


def f64(x):
    return np.asarray(x).astype(np.float64)


E2M1 = np.array([0.0, 0.5, 1.0, 1.5, 2.0, 3.0, 4.0, 6.0, -0.0, -0.5, -1.0, -1.5, -2.0, -3.0, -4.0, -6.0])


def pack_weight(w, fmt):
    k, n = w.shape
    w = f64(bf(w)).reshape(k // 32, 32, n)
    amax = np.abs(w).max(1)
    if fmt == "e4m3":
        byte = np.frexp(amax)[1] - 1 + 127 - 7
    else:
        mant, ex = np.frexp(amax / 6.0)
        byte = np.where(mant > 0.5, ex, ex - 1) + 127
    byte = np.clip(np.where(amax > 0, byte, 1), 1, 254)
    scaled = (w * np.exp2(127.0 - byte)[:, None, :]).reshape(k, n).astype(np.float32)
    by_word = np.ascontiguousarray(scaled.reshape(k // 512, 128, 4, n).transpose(0, 1, 3, 2))
    if fmt == "e4m3":
        words = by_word.astype(ml_dtypes.float8_e4m3fn).view(np.uint8)
    else:
        c = by_word.astype(ml_dtypes.float4_e2m1fn).view(np.uint8) & 0xF
        words = c[..., 0::2] | (c[..., 1::2] << 4)
    return np.ascontiguousarray(words), np.ascontiguousarray(byte.astype(np.uint8).reshape(k // 512, 16, n))


def unpack_weight(words, scales, fmt):
    g, p, n, _ = words.shape
    if fmt == "e4m3":
        vals = np.ascontiguousarray(words).view(ml_dtypes.float8_e4m3fn).astype(np.float64)
    else:
        nib = np.empty((g, p, n, 4), np.uint8)
        nib[..., 0::2] = words & 0xF
        nib[..., 1::2] = words >> 4
        vals = E2M1[nib]
    vals = vals * np.repeat(np.exp2(scales.astype(np.float64) - 127.0), 8, axis=1)[..., None]
    return vals.transpose(0, 1, 3, 2).reshape(g * 512, n)


B, I, H = 1024, 512, 512
FMT = "e4m3"


def sigmoid(v):
    return 1.0 / (1.0 + np.exp(-v))


def setup_inputs():
    s = mx_kscale(I)
    x = bf(np.random.standard_normal((B, I)) * s)
    h_prev = bf(np.random.standard_normal((B, H)))
    c_prev = bf(np.random.standard_normal((B, H)))
    w_ih = np.random.standard_normal((4 * H, I)) * 1.0 / np.sqrt(I) / s[None, :]
    w_ih_words, w_ih_scales = pack_weight(np.ascontiguousarray(w_ih.T), FMT)
    w_hh = bf(np.random.standard_normal((4 * H, H)) * 1.0 / np.sqrt(H))
    bias_ih = bf(np.random.standard_normal(4 * H) * 0.5)
    bias_hh = bf(np.random.standard_normal(4 * H) * 0.5)
    return {"x": x,
            "h_prev": h_prev,
            "c_prev": c_prev,
            "w_ih_words": w_ih_words,
            "w_ih_scales": w_ih_scales,
            "w_hh": w_hh,
            "bias_ih": bias_ih,
            "bias_hh": bias_hh}


def reference(x, h_prev, c_prev, w_ih_words, w_ih_scales, w_hh, bias_ih, bias_hh):
    gates = (mxq(f64(x), 1, "e4m3") @ unpack_weight(w_ih_words, w_ih_scales, FMT)) + f64(bias_ih) + f64(h_prev) @ f64(w_hh).T + f64(bias_hh)
    i_g, f_g, g_g, o_g = np.split(gates, 4, axis=1)
    i_g = sigmoid(i_g)
    f_g = sigmoid(f_g)
    g_g = np.tanh(g_g)
    o_g = sigmoid(o_g)
    c_new = f_g * f64(c_prev) + i_g * g_g
    h_new = o_g * np.tanh(c_new)
    return (h_new, c_new)

@@ -1,0 +1,191 @@
+from contextlib import ExitStack
+
+import concourse.mybir as mybir
+from concourse.masks import make_identity
+
+BF16 = mybir.dt.bfloat16
+F32 = mybir.dt.float32
+I32 = mybir.dt.int32
+U32 = mybir.dt.uint32
+U8 = mybir.dt.uint8
+FP8X4 = mybir.dt.float8_e4m3fn_x4
+ADD = mybir.AluOpType.add
+MULT = mybir.AluOpType.mult
+SIGMOID = mybir.ActivationFunctionType.Sigmoid
+TANH = mybir.ActivationFunctionType.Tanh
+
+P = 128
+BATCH = 1024
+FEAT = 512
+N_GATES = 4
+GATE_COLS = N_GATES * FEAT
+TILES = BATCH // P
+K_CHUNKS = FEAT // P
+PAIR = 2
+MX_AHEAD = 2
+
+FLOPS = 2 * BATCH * FEAT * GATE_COLS * 2
+
+
+def tile_int8lstmcell_kernel(
+    tc, x, h_prev, c_prev, w_ih_words, w_ih_scales, w_hh, bias_ih, bias_hh, out_0, out_1
+):
+    nc = tc.nc
+    with ExitStack() as stack:
+        keep = stack.enter_context(tc.tile_pool(name="keep", bufs=1))
+        psum_mx = stack.enter_context(tc.psum_pool(name="psum_mx", bufs=2))
+        psum_tp = stack.enter_context(tc.psum_pool(name="psum_tp", bufs=2))
+        psum_pl = stack.enter_context(tc.psum_pool(name="psum_pl", bufs=4))
+
+        x_view = x.rearrange("(p b) k -> p b k", b=TILES)
+        h_view = h_prev.rearrange("(p b) k -> p b k", b=TILES)
+        c_view = c_prev.rearrange("(p b) k -> p b k", b=TILES)
+        h_new_view = out_0.rearrange("(p b) n -> p b n", b=TILES)
+        c_new_view = out_1.rearrange("(p b) n -> p b n", b=TILES)
+        w_hh_view = w_hh.rearrange("(j p) k -> p j k", p=P)
+        words_view = w_ih_words[0].rearrange("p n t -> p (n t)")
+
+        x_sb = keep.tile([P, TILES, FEAT], BF16)
+        h_sb = keep.tile([P, TILES, FEAT], BF16)
+        c_sb = keep.tile([P, TILES, FEAT], BF16)
+        w_sb = keep.tile([P, GATE_COLS // P, FEAT], BF16)
+        w_words = keep.tile([P, GATE_COLS], U32, align_bytes=64)
+        w_plane = keep.tile([P, GATE_COLS], U8, align_bytes=64)
+        bias_rows = keep.tile([P, GATE_COLS], BF16)
+        bias_all = keep.tile([P, GATE_COLS], F32)
+        ones = keep.tile([P, P], BF16)
+        ident_bf = keep.tile([P, P], BF16)
+        ident_f32 = keep.tile([P, P], F32)
+        warm = keep.tile([P, 1], F32)
+        x_grouped = keep.tile([P, BATCH * 4], BF16, align_bytes=64)
+        x_codes = keep.tile([P, BATCH], U32, align_bytes=64)
+        x_plane = keep.tile([P, BATCH], U8, align_bytes=64)
+        h_t = keep.tile([P, K_CHUNKS, BATCH], BF16)
+        w_t = keep.tile([P, K_CHUNKS, GATE_COLS], BF16)
+        gates = keep.tile([P, TILES, GATE_COLS], F32)
+        c_new = keep.tile([P, TILES, FEAT], F32)
+        h_new = keep.tile([P, TILES, FEAT], F32)
+
+        nc.vector.memset(warm[:], 0.0)
+        nc.vector.memset(bias_rows[:].bitcast(I32), 0)
+        nc.vector.memset(w_plane[:].bitcast(I32), 0)
+        nc.vector.memset(ones[:], 1.0)
+        make_identity(nc, ident_f32[:])
+        make_identity(nc, ident_bf[:])
+        nc.scalar.activation(out=warm[:], in_=warm[:], func=SIGMOID)
+
+        nc.scalar.dma_start(out=bias_rows[0:1, :], in_=bias_ih.rearrange("(o n) -> o n", o=1))
+        nc.scalar.dma_start(out=bias_rows[1:2, :], in_=bias_hh.rearrange("(o n) -> o n", o=1))
+        for b in range(0, TILES, PAIR):
+            nc.sync.dma_start(out=x_sb[:, b : b + PAIR, :], in_=x_view[:, b : b + PAIR, :])
+        for q in range(4):
+            nc.sync.dma_start(
+                out=w_plane[32 * q : 32 * q + 4, :].bitcast(I32),
+                in_=w_ih_scales[0, 4 * q : 4 * q + 4, :].bitcast(I32),
+            )
+        for g in range(N_GATES):
+            nc.sync.dma_start(
+                out=w_words[:, g * FEAT : (g + 1) * FEAT].bitcast(I32),
+                in_=words_view[:, g * FEAT * 4 : (g + 1) * FEAT * 4].bitcast(I32),
+            )
+        nc.sync.dma_start(out=h_sb[:, 0:PAIR, :], in_=h_view[:, 0:PAIR, :])
+        for g in range(N_GATES):
+            nc.sync.dma_start(out=w_sb[:, 4 * g : 4 * g + 4, :], in_=w_hh_view[:, 4 * g : 4 * g + 4, :])
+        for b in range(PAIR, TILES, PAIR):
+            nc.sync.dma_start(out=h_sb[:, b : b + PAIR, :], in_=h_view[:, b : b + PAIR, :])
+        for b in range(0, TILES, PAIR):
+            nc.sync.dma_start(out=c_sb[:, b : b + PAIR, :], in_=c_view[:, b : b + PAIR, :])
+
+        for g in range(N_GATES):
+            cols = slice(g * FEAT, (g + 1) * FEAT)
+            bias_ps = psum_pl.tile([P, FEAT], F32, tag="pl")
+            nc.tensor.matmul(out=bias_ps[:], lhsT=ones[:], rhs=bias_rows[:, cols], start=True, stop=True)
+            nc.scalar.copy(out=bias_all[:, cols], in_=bias_ps[:])
+
+        grouped_words = x_grouped[:].bitcast(F32).rearrange("p (b r u) -> p b r u", b=TILES, u=2)
+        for b0 in range(0, TILES, PAIR):
+            x_ps = psum_tp.tile([P, PAIR, 2, P], F32, tag="tp")
+            for t in range(PAIR):
+                words = x_sb[:, b0 + t, :].bitcast(F32)
+                for u in range(2):
+                    nc.tensor.transpose(x_ps[:, t, u, :], words[:, u : FEAT // 2 : 2], ident_f32[:])
+            nc.vector.tensor_copy(
+                out=grouped_words[:, b0 : b0 + PAIR, :, :], in_=x_ps[:].rearrange("p t u r -> p t r u")
+            )
+            rows = slice(b0 * P, (b0 + PAIR) * P)
+            nc.vector.quantize_mx(
+                out=x_codes[:, rows].bitcast(FP8X4),
+                scales=x_plane[:, rows],
+                in_=x_grouped[:, b0 * P * 4 : (b0 + PAIR) * P * 4],
+            )
+
+        def mx_product(b):
+            rows = slice(b * P, (b + 1) * P)
+            for g in range(N_GATES):
+                cols = slice(g * FEAT, (g + 1) * FEAT)
+                mx_ps = psum_mx.tile([P, FEAT], F32, tag="mx")
+                nc.tensor.matmul_mx(
+                    out=mx_ps[:],
+                    lhsT=x_codes[:, rows].bitcast(FP8X4),
+                    lhsT_scale=x_plane[:, rows],
+                    rhs=w_words[:, cols].bitcast(FP8X4),
+                    rhs_scale=w_plane[:, cols],
+                    start=True,
+                    stop=True,
+                )
+                nc.vector.tensor_tensor(out=gates[:, b, cols], in0=mx_ps[:], in1=bias_all[:, cols], op=ADD)
+
+        def transpose_w(j):
+            w_ps = psum_tp.tile([P, K_CHUNKS, P], BF16, tag="tp")
+            for kc in range(K_CHUNKS):
+                nc.tensor.transpose(w_ps[:, kc, :], w_sb[:, j, kc * P : (kc + 1) * P], ident_bf[:])
+            nc.scalar.copy(out=w_t[:, :, j * P : (j + 1) * P], in_=w_ps[:])
+
+        def transpose_h(b):
+            h_ps = psum_tp.tile([P, K_CHUNKS, P], BF16, tag="tp")
+            for kc in range(K_CHUNKS):
+                nc.tensor.transpose(h_ps[:, kc, :], h_sb[:, b, kc * P : (kc + 1) * P], ident_bf[:])
+            nc.scalar.copy(out=h_t[:, :, b * P : (b + 1) * P], in_=h_ps[:])
+
+        def plain_product(b):
+            for g in range(N_GATES):
+                cols = slice(g * FEAT, (g + 1) * FEAT)
+                pl_ps = psum_pl.tile([P, FEAT], F32, tag="pl")
+                for kc in range(K_CHUNKS):
+                    nc.tensor.matmul(
+                        out=pl_ps[:],
+                        lhsT=h_t[:, kc, b * P : (b + 1) * P],
+                        rhs=w_t[:, kc, cols],
+                        start=(kc == 0),
+                        stop=(kc == K_CHUNKS - 1),
+                    )
+                nc.vector.tensor_tensor(out=gates[:, b, cols], in0=pl_ps[:], in1=gates[:, b, cols], op=ADD)
+
+        def cell(b):
+            gate_i = gates[:, b, 0 * FEAT : 1 * FEAT]
+            gate_f = gates[:, b, 1 * FEAT : 2 * FEAT]
+            gate_g = gates[:, b, 2 * FEAT : 3 * FEAT]
+            gate_o = gates[:, b, 3 * FEAT : 4 * FEAT]
+            gate_if = gates[:, b, 0 : 2 * FEAT]
+            nc.scalar.activation(out=gate_if, in_=gate_if, func=SIGMOID)
+            nc.scalar.activation(out=gate_g, in_=gate_g, func=TANH)
+            nc.scalar.activation(out=gate_o, in_=gate_o, func=SIGMOID)
+            nc.gpsimd.tensor_tensor(out=gate_f, in0=gate_f, in1=c_sb[:, b, :], op=MULT)
+            nc.gpsimd.tensor_tensor(out=gate_i, in0=gate_i, in1=gate_g, op=MULT)
+            nc.gpsimd.tensor_tensor(out=c_new[:, b, :], in0=gate_f, in1=gate_i, op=ADD)
+            nc.sync.dma_start(out=c_new_view[:, b, :], in_=c_new[:, b, :])
+            nc.scalar.activation(out=gate_g, in_=c_new[:, b, :], func=TANH)
+            nc.gpsimd.tensor_tensor(out=h_new[:, b, :], in0=gate_o, in1=gate_g, op=MULT)
+            nc.sync.dma_start(out=h_new_view[:, b, :], in_=h_new[:, b, :])
+
+        for b in range(MX_AHEAD):
+            mx_product(b)
+            transpose_h(b)
+        for j in range(GATE_COLS // P):
+            transpose_w(j)
+        for b in range(TILES):
+            if b + MX_AHEAD < TILES:
+                transpose_h(b + MX_AHEAD)
+                mx_product(b + MX_AHEAD)
+            plain_product(b)
+            cell(b)

@@ -22,6 +22,8 @@ GATE_COLS = N_GATES * FEAT
 TILES = BATCH // P
 K_CHUNKS = FEAT // P
 PAIR = 2
+PAIRS = TILES // PAIR
+ROW_TILES = FEAT // P
 MX_AHEAD = 2
 
 FLOPS = 2 * BATCH * FEAT * GATE_COLS * 2
@@ -34,8 +36,9 @@ def tile_int8lstmcell_kernel(
     with ExitStack() as stack:
         keep = stack.enter_context(tc.tile_pool(name="keep", bufs=1))
         psum_mx = stack.enter_context(tc.psum_pool(name="psum_mx", bufs=2))
-        psum_tp = stack.enter_context(tc.psum_pool(name="psum_tp", bufs=2))
-        psum_pl = stack.enter_context(tc.psum_pool(name="psum_pl", bufs=4))
+        psum_tp = stack.enter_context(tc.psum_pool(name="psum_tp", bufs=3))
+        psum_pl = stack.enter_context(tc.psum_pool(name="psum_pl", bufs=3))
+        stack.enter_context(tc.manual_schedule())
 
         x_view = x.rearrange("(p b) k -> p b k", b=TILES)
         h_view = h_prev.rearrange("(p b) k -> p b k", b=TILES)
@@ -48,7 +51,7 @@ def tile_int8lstmcell_kernel(
         x_sb = keep.tile([P, TILES, FEAT], BF16)
         h_sb = keep.tile([P, TILES, FEAT], BF16)
         c_sb = keep.tile([P, TILES, FEAT], BF16)
-        w_sb = keep.tile([P, GATE_COLS // P, FEAT], BF16)
+        w_sb = keep.tile([P, N_GATES * ROW_TILES, FEAT], BF16)
         w_words = keep.tile([P, GATE_COLS], U32, align_bytes=64)
         w_plane = keep.tile([P, GATE_COLS], U8, align_bytes=64)
         bias_rows = keep.tile([P, GATE_COLS], BF16)
@@ -66,6 +69,9 @@ def tile_int8lstmcell_kernel(
         c_new = keep.tile([P, TILES, FEAT], F32)
         h_new = keep.tile([P, TILES, FEAT], F32)
 
+        def gate(b, g):
+            return gates[:, b, g * FEAT : (g + 1) * FEAT]
+
         nc.vector.memset(warm[:], 0.0)
         nc.vector.memset(bias_rows[:].bitcast(I32), 0)
         nc.vector.memset(w_plane[:].bitcast(I32), 0)
@@ -74,27 +80,31 @@ def tile_int8lstmcell_kernel(
         make_identity(nc, ident_bf[:])
         nc.scalar.activation(out=warm[:], in_=warm[:], func=SIGMOID)
 
+        def load_pair(dst, src, q):
+            nc.sync.dma_start(out=dst[:, q * PAIR : (q + 1) * PAIR, :], in_=src[:, q * PAIR : (q + 1) * PAIR, :])
+
         nc.scalar.dma_start(out=bias_rows[0:1, :], in_=bias_ih.rearrange("(o n) -> o n", o=1))
         nc.scalar.dma_start(out=bias_rows[1:2, :], in_=bias_hh.rearrange("(o n) -> o n", o=1))
-        for b in range(0, TILES, PAIR):
-            nc.sync.dma_start(out=x_sb[:, b : b + PAIR, :], in_=x_view[:, b : b + PAIR, :])
-        for q in range(4):
+        for q in range(PAIRS):
+            load_pair(x_sb, x_view, q)
+        load_pair(h_sb, h_view, 0)
+        for s in range(4):
             nc.sync.dma_start(
-                out=w_plane[32 * q : 32 * q + 4, :].bitcast(I32),
-                in_=w_ih_scales[0, 4 * q : 4 * q + 4, :].bitcast(I32),
+                out=w_plane[32 * s : 32 * s + 4, :].bitcast(I32),
+                in_=w_ih_scales[0, 4 * s : 4 * s + 4, :].bitcast(I32),
             )
         for g in range(N_GATES):
             nc.sync.dma_start(
                 out=w_words[:, g * FEAT : (g + 1) * FEAT].bitcast(I32),
                 in_=words_view[:, g * FEAT * 4 : (g + 1) * FEAT * 4].bitcast(I32),
             )
-        nc.sync.dma_start(out=h_sb[:, 0:PAIR, :], in_=h_view[:, 0:PAIR, :])
         for g in range(N_GATES):
-            nc.sync.dma_start(out=w_sb[:, 4 * g : 4 * g + 4, :], in_=w_hh_view[:, 4 * g : 4 * g + 4, :])
-        for b in range(PAIR, TILES, PAIR):
-            nc.sync.dma_start(out=h_sb[:, b : b + PAIR, :], in_=h_view[:, b : b + PAIR, :])
-        for b in range(0, TILES, PAIR):
-            nc.sync.dma_start(out=c_sb[:, b : b + PAIR, :], in_=c_view[:, b : b + PAIR, :])
+            row_tiles = slice(g * ROW_TILES, (g + 1) * ROW_TILES)
+            nc.sync.dma_start(out=w_sb[:, row_tiles, :], in_=w_hh_view[:, row_tiles, :])
+        for q in range(PAIRS):
+            if q + 1 < PAIRS:
+                load_pair(h_sb, h_view, q + 1)
+            load_pair(c_sb, c_view, q)
 
         for g in range(N_GATES):
             cols = slice(g * FEAT, (g + 1) * FEAT)
@@ -103,26 +113,34 @@ def tile_int8lstmcell_kernel(
             nc.scalar.copy(out=bias_all[:, cols], in_=bias_ps[:])
 
         grouped_words = x_grouped[:].bitcast(F32).rearrange("p (b r u) -> p b r u", b=TILES, u=2)
-        for b0 in range(0, TILES, PAIR):
-            x_ps = psum_tp.tile([P, PAIR, 2, P], F32, tag="tp")
-            for t in range(PAIR):
-                words = x_sb[:, b0 + t, :].bitcast(F32)
-                for u in range(2):
-                    nc.tensor.transpose(x_ps[:, t, u, :], words[:, u : FEAT // 2 : 2], ident_f32[:])
-            nc.vector.tensor_copy(
-                out=grouped_words[:, b0 : b0 + PAIR, :, :], in_=x_ps[:].rearrange("p t u r -> p t r u")
-            )
-            rows = slice(b0 * P, (b0 + PAIR) * P)
+
+        def quantise_pair(q):
+            rows = slice(q * PAIR * P, (q + 1) * PAIR * P)
             nc.vector.quantize_mx(
                 out=x_codes[:, rows].bitcast(FP8X4),
                 scales=x_plane[:, rows],
-                in_=x_grouped[:, b0 * P * 4 : (b0 + PAIR) * P * 4],
+                in_=x_grouped[:, q * PAIR * P * 4 : (q + 1) * PAIR * P * 4],
             )
 
-        def mx_product(b):
-            rows = slice(b * P, (b + 1) * P)
-            for g in range(N_GATES):
-                cols = slice(g * FEAT, (g + 1) * FEAT)
+        for q in range(PAIRS):
+            x_ps = psum_tp.tile([P, PAIR, 2, P], F32, tag="tp")
+            for t in range(PAIR):
+                words = x_sb[:, q * PAIR + t, :].bitcast(F32)
+                for u in range(2):
+                    nc.tensor.transpose(x_ps[:, t, u, :], words[:, u : FEAT // 2 : 2], ident_f32[:])
+            nc.vector.tensor_copy(
+                out=grouped_words[:, q * PAIR : (q + 1) * PAIR, :, :], in_=x_ps[:].rearrange("p t u r -> p t r u")
+            )
+            if q > 0:
+                quantise_pair(q - 1)
+        quantise_pair(PAIRS - 1)
+
+        def mx_block(block):
+            q, g = divmod(block, N_GATES)
+            cols = slice(g * FEAT, (g + 1) * FEAT)
+            for t in range(PAIR):
+                b = q * PAIR + t
+                rows = slice(b * P, (b + 1) * P)
                 mx_ps = psum_mx.tile([P, FEAT], F32, tag="mx")
                 nc.tensor.matmul_mx(
                     out=mx_ps[:],
@@ -133,59 +151,86 @@ def tile_int8lstmcell_kernel(
                     start=True,
                     stop=True,
                 )
-                nc.vector.tensor_tensor(out=gates[:, b, cols], in0=mx_ps[:], in1=bias_all[:, cols], op=ADD)
+                nc.vector.tensor_tensor(out=gate(b, g), in0=mx_ps[:], in1=bias_all[:, cols], op=ADD)
 
-        def transpose_w(j):
-            w_ps = psum_tp.tile([P, K_CHUNKS, P], BF16, tag="tp")
-            for kc in range(K_CHUNKS):
-                nc.tensor.transpose(w_ps[:, kc, :], w_sb[:, j, kc * P : (kc + 1) * P], ident_bf[:])
-            nc.scalar.copy(out=w_t[:, :, j * P : (j + 1) * P], in_=w_ps[:])
+        def w_flips(g):
+            return [
+                (w_sb[:, j, :], w_t[:, :, j * P : (j + 1) * P])
+                for j in range(g * ROW_TILES, (g + 1) * ROW_TILES)
+            ]
 
-        def transpose_h(b):
-            h_ps = psum_tp.tile([P, K_CHUNKS, P], BF16, tag="tp")
-            for kc in range(K_CHUNKS):
-                nc.tensor.transpose(h_ps[:, kc, :], h_sb[:, b, kc * P : (kc + 1) * P], ident_bf[:])
-            nc.scalar.copy(out=h_t[:, :, b * P : (b + 1) * P], in_=h_ps[:])
+        def h_flips(q):
+            return [(h_sb[:, b, :], h_t[:, :, b * P : (b + 1) * P]) for b in range(q * PAIR, (q + 1) * PAIR)]
 
-        def plain_product(b):
-            for g in range(N_GATES):
-                cols = slice(g * FEAT, (g + 1) * FEAT)
-                pl_ps = psum_pl.tile([P, FEAT], F32, tag="pl")
-                for kc in range(K_CHUNKS):
-                    nc.tensor.matmul(
-                        out=pl_ps[:],
-                        lhsT=h_t[:, kc, b * P : (b + 1) * P],
-                        rhs=w_t[:, kc, cols],
-                        start=(kc == 0),
-                        stop=(kc == K_CHUNKS - 1),
-                    )
-                nc.vector.tensor_tensor(out=gates[:, b, cols], in0=pl_ps[:], in1=gates[:, b, cols], op=ADD)
+        def flip_chunks(flip_ps, src, chunks):
+            for kc in chunks:
+                nc.tensor.transpose(flip_ps[:, kc, :], src[:, kc * P : (kc + 1) * P], ident_bf[:])
 
-        def cell(b):
-            gate_i = gates[:, b, 0 * FEAT : 1 * FEAT]
-            gate_f = gates[:, b, 1 * FEAT : 2 * FEAT]
-            gate_g = gates[:, b, 2 * FEAT : 3 * FEAT]
-            gate_o = gates[:, b, 3 * FEAT : 4 * FEAT]
-            gate_if = gates[:, b, 0 : 2 * FEAT]
-            nc.scalar.activation(out=gate_if, in_=gate_if, func=SIGMOID)
-            nc.scalar.activation(out=gate_g, in_=gate_g, func=TANH)
-            nc.scalar.activation(out=gate_o, in_=gate_o, func=SIGMOID)
-            nc.gpsimd.tensor_tensor(out=gate_f, in0=gate_f, in1=c_sb[:, b, :], op=MULT)
-            nc.gpsimd.tensor_tensor(out=gate_i, in0=gate_i, in1=gate_g, op=MULT)
-            nc.gpsimd.tensor_tensor(out=c_new[:, b, :], in0=gate_f, in1=gate_i, op=ADD)
-            nc.sync.dma_start(out=c_new_view[:, b, :], in_=c_new[:, b, :])
-            nc.scalar.activation(out=gate_g, in_=c_new[:, b, :], func=TANH)
-            nc.gpsimd.tensor_tensor(out=h_new[:, b, :], in0=gate_o, in1=gate_g, op=MULT)
+        def flip_now(flips):
+            for src, dst in flips:
+                flip_ps = psum_tp.tile([P, K_CHUNKS, P], BF16, tag="tp")
+                flip_chunks(flip_ps, src, range(K_CHUNKS))
+                nc.scalar.copy(out=dst, in_=flip_ps[:])
+
+        def finish_tile(b):
+            nc.scalar.activation(out=gate(b, 2), in_=c_new[:, b, :], func=TANH)
+            nc.vector.tensor_tensor(out=h_new[:, b, :], in0=gate(b, 3), in1=gate(b, 2), op=MULT)
             nc.sync.dma_start(out=h_new_view[:, b, :], in_=h_new[:, b, :])
 
-        for b in range(MX_AHEAD):
-            mx_product(b)
-            transpose_h(b)
-        for j in range(GATE_COLS // P):
-            transpose_w(j)
-        for b in range(TILES):
-            if b + MX_AHEAD < TILES:
-                transpose_h(b + MX_AHEAD)
-                mx_product(b + MX_AHEAD)
-            plain_product(b)
-            cell(b)
+        flip_now(h_flips(0))
+        for block in range(MX_AHEAD):
+            mx_block(block)
+        flip_now(w_flips(0))
+
+        for q in range(PAIRS):
+            for g in range(N_GATES):
+                block = q * N_GATES + g
+                cols = slice(g * FEAT, (g + 1) * FEAT)
+                if block + MX_AHEAD < PAIRS * N_GATES:
+                    mx_block(block + MX_AHEAD)
+                if q > 0 and g < PAIR:
+                    finish_tile((q - 1) * PAIR + g)
+
+                if q == 0 and g + 1 < N_GATES:
+                    flips = w_flips(g + 1)
+                elif g == N_GATES - 1 and q + 1 < PAIRS:
+                    flips = h_flips(q + 1)
+                else:
+                    flips = []
+                sums = []
+                for t in range(PAIR):
+                    b = q * PAIR + t
+                    pl_ps = psum_pl.tile([P, FEAT], F32, tag="pl")
+                    sums.append(pl_ps)
+                    for kc in range(K_CHUNKS):
+                        nc.tensor.matmul(
+                            out=pl_ps[:],
+                            lhsT=h_t[:, kc, b * P : (b + 1) * P],
+                            rhs=w_t[:, kc, cols],
+                            start=(kc == 0),
+                            stop=(kc == K_CHUNKS - 1),
+                        )
+                        rider, half = divmod(t * K_CHUNKS + kc, 2)
+                        if rider < len(flips):
+                            src, dst = flips[rider]
+                            if half == 0:
+                                flip_ps = psum_tp.tile([P, K_CHUNKS, P], BF16, tag="tp")
+                            flip_chunks(flip_ps, src, range(2 * half, 2 * half + 2))
+                            if half == 1:
+                                nc.scalar.copy(out=dst, in_=flip_ps[:])
+                for t in range(PAIR):
+                    b = q * PAIR + t
+                    nc.vector.tensor_tensor(out=gate(b, g), in0=sums[t][:], in1=gate(b, g), op=ADD)
+                for t in range(PAIR):
+                    b = q * PAIR + t
+                    nc.scalar.activation(out=gate(b, g), in_=gate(b, g), func=(TANH if g == 2 else SIGMOID))
+                for t in range(PAIR):
+                    b = q * PAIR + t
+                    if g == 1:
+                        nc.gpsimd.tensor_tensor(out=gate(b, 1), in0=gate(b, 1), in1=c_sb[:, b, :], op=MULT)
+                    if g == 2:
+                        nc.gpsimd.tensor_tensor(out=gate(b, 0), in0=gate(b, 0), in1=gate(b, 2), op=MULT)
+                        nc.gpsimd.tensor_tensor(out=c_new[:, b, :], in0=gate(b, 1), in1=gate(b, 0), op=ADD)
+                        nc.sync.dma_start(out=c_new_view[:, b, :], in_=c_new[:, b, :])
+        for t in range(PAIR):
+            finish_tile((PAIRS - 1) * PAIR + t)

@@ -24,7 +24,8 @@ K_CHUNKS = FEAT // P
 PAIR = 2
 PAIRS = TILES // PAIR
 ROW_TILES = FEAT // P
-MX_AHEAD = 2
+BLOCKS = PAIRS * N_GATES
+X_AHEAD = 2
 
 FLOPS = 2 * BATCH * FEAT * GATE_COLS * 2
 
@@ -38,7 +39,6 @@ def tile_int8lstmcell_kernel(
         psum_mx = stack.enter_context(tc.psum_pool(name="psum_mx", bufs=2))
         psum_tp = stack.enter_context(tc.psum_pool(name="psum_tp", bufs=3))
         psum_pl = stack.enter_context(tc.psum_pool(name="psum_pl", bufs=3))
-        stack.enter_context(tc.manual_schedule())
 
         x_view = x.rearrange("(p b) k -> p b k", b=TILES)
         h_view = h_prev.rearrange("(p b) k -> p b k", b=TILES)
@@ -72,10 +72,10 @@ def tile_int8lstmcell_kernel(
         def gate(b, g):
             return gates[:, b, g * FEAT : (g + 1) * FEAT]
 
-        nc.vector.memset(warm[:], 0.0)
         nc.vector.memset(bias_rows[:].bitcast(I32), 0)
         nc.vector.memset(w_plane[:].bitcast(I32), 0)
         nc.vector.memset(ones[:], 1.0)
+        nc.vector.memset(warm[:], 0.0)
         make_identity(nc, ident_f32[:])
         make_identity(nc, ident_bf[:])
         nc.scalar.activation(out=warm[:], in_=warm[:], func=SIGMOID)
@@ -83,57 +83,59 @@ def tile_int8lstmcell_kernel(
         def load_pair(dst, src, q):
             nc.sync.dma_start(out=dst[:, q * PAIR : (q + 1) * PAIR, :], in_=src[:, q * PAIR : (q + 1) * PAIR, :])
 
-        nc.scalar.dma_start(out=bias_rows[0:1, :], in_=bias_ih.rearrange("(o n) -> o n", o=1))
-        nc.scalar.dma_start(out=bias_rows[1:2, :], in_=bias_hh.rearrange("(o n) -> o n", o=1))
-        for q in range(PAIRS):
+        def load_w_hh(g):
+            row_tiles = slice(g * ROW_TILES, (g + 1) * ROW_TILES)
+            nc.sync.dma_start(out=w_sb[:, row_tiles, :], in_=w_hh_view[:, row_tiles, :])
+
+        def load_words(g):
+            nc.sync.dma_start(
+                out=w_words[:, g * FEAT : (g + 1) * FEAT].bitcast(I32),
+                in_=words_view[:, g * FEAT * 4 : (g + 1) * FEAT * 4].bitcast(I32),
+            )
+
+        for q in range(X_AHEAD):
             load_pair(x_sb, x_view, q)
         load_pair(h_sb, h_view, 0)
+        load_w_hh(0)
+        nc.sync.dma_start(out=bias_rows[0:1, :], in_=bias_ih.rearrange("(o n) -> o n", o=1))
+        nc.sync.dma_start(out=bias_rows[1:2, :], in_=bias_hh.rearrange("(o n) -> o n", o=1))
         for s in range(4):
             nc.sync.dma_start(
                 out=w_plane[32 * s : 32 * s + 4, :].bitcast(I32),
                 in_=w_ih_scales[0, 4 * s : 4 * s + 4, :].bitcast(I32),
             )
-        for g in range(N_GATES):
-            nc.sync.dma_start(
-                out=w_words[:, g * FEAT : (g + 1) * FEAT].bitcast(I32),
-                in_=words_view[:, g * FEAT * 4 : (g + 1) * FEAT * 4].bitcast(I32),
-            )
-        for g in range(N_GATES):
-            row_tiles = slice(g * ROW_TILES, (g + 1) * ROW_TILES)
-            nc.sync.dma_start(out=w_sb[:, row_tiles, :], in_=w_hh_view[:, row_tiles, :])
+        load_words(0)
+        for g in range(1, N_GATES):
+            load_w_hh(g)
+            load_words(g)
         for q in range(PAIRS):
             if q + 1 < PAIRS:
                 load_pair(h_sb, h_view, q + 1)
             load_pair(c_sb, c_view, q)
-
-        for g in range(N_GATES):
-            cols = slice(g * FEAT, (g + 1) * FEAT)
-            bias_ps = psum_pl.tile([P, FEAT], F32, tag="pl")
-            nc.tensor.matmul(out=bias_ps[:], lhsT=ones[:], rhs=bias_rows[:, cols], start=True, stop=True)
-            nc.scalar.copy(out=bias_all[:, cols], in_=bias_ps[:])
+            if q + X_AHEAD < PAIRS:
+                load_pair(x_sb, x_view, q + X_AHEAD)
 
         grouped_words = x_grouped[:].bitcast(F32).rearrange("p (b r u) -> p b r u", b=TILES, u=2)
 
-        def quantise_pair(q):
+        def x_transposes(x_ps, q):
+            return [
+                (x_ps[:, t, u, :], x_sb[:, q * PAIR + t, :].bitcast(F32)[:, u : FEAT // 2 : 2], ident_f32[:])
+                for t in range(PAIR)
+                for u in range(2)
+            ]
+
+        def x_copy(x_ps, q):
+            nc.vector.tensor_copy(
+                out=grouped_words[:, q * PAIR : (q + 1) * PAIR, :, :], in_=x_ps[:].rearrange("p t u r -> p t r u")
+            )
+
+        def x_quantise(q):
             rows = slice(q * PAIR * P, (q + 1) * PAIR * P)
             nc.vector.quantize_mx(
                 out=x_codes[:, rows].bitcast(FP8X4),
                 scales=x_plane[:, rows],
                 in_=x_grouped[:, q * PAIR * P * 4 : (q + 1) * PAIR * P * 4],
             )
-
-        for q in range(PAIRS):
-            x_ps = psum_tp.tile([P, PAIR, 2, P], F32, tag="tp")
-            for t in range(PAIR):
-                words = x_sb[:, q * PAIR + t, :].bitcast(F32)
-                for u in range(2):
-                    nc.tensor.transpose(x_ps[:, t, u, :], words[:, u : FEAT // 2 : 2], ident_f32[:])
-            nc.vector.tensor_copy(
-                out=grouped_words[:, q * PAIR : (q + 1) * PAIR, :, :], in_=x_ps[:].rearrange("p t u r -> p t r u")
-            )
-            if q > 0:
-                quantise_pair(q - 1)
-        quantise_pair(PAIRS - 1)
 
         def mx_block(block):
             q, g = divmod(block, N_GATES)
@@ -153,74 +155,90 @@ def tile_int8lstmcell_kernel(
                 )
                 nc.vector.tensor_tensor(out=gate(b, g), in0=mx_ps[:], in1=bias_all[:, cols], op=ADD)
 
-        def w_flips(g):
-            return [
-                (w_sb[:, j, :], w_t[:, :, j * P : (j + 1) * P])
-                for j in range(g * ROW_TILES, (g + 1) * ROW_TILES)
-            ]
+        def w_flip(j):
+            return (w_sb[:, j, :], w_t[:, :, j * P : (j + 1) * P])
 
-        def h_flips(q):
-            return [(h_sb[:, b, :], h_t[:, :, b * P : (b + 1) * P]) for b in range(q * PAIR, (q + 1) * PAIR)]
+        def h_flip(b):
+            return (h_sb[:, b, :], h_t[:, :, b * P : (b + 1) * P])
 
-        def flip_chunks(flip_ps, src, chunks):
-            for kc in chunks:
-                nc.tensor.transpose(flip_ps[:, kc, :], src[:, kc * P : (kc + 1) * P], ident_bf[:])
+        def flip_transposes(flip_ps, flip):
+            return [(flip_ps[:, kc, :], flip[0][:, kc * P : (kc + 1) * P], ident_bf[:]) for kc in range(K_CHUNKS)]
 
-        def flip_now(flips):
-            for src, dst in flips:
-                flip_ps = psum_tp.tile([P, K_CHUNKS, P], BF16, tag="tp")
-                flip_chunks(flip_ps, src, range(K_CHUNKS))
-                nc.scalar.copy(out=dst, in_=flip_ps[:])
+        def plain_group(b, g, riders):
+            share = len(riders) // K_CHUNKS
+            pl_ps = psum_pl.tile([P, FEAT], F32, tag="pl")
+            for kc in range(K_CHUNKS):
+                nc.tensor.matmul(
+                    out=pl_ps[:],
+                    lhsT=h_t[:, kc, b * P : (b + 1) * P],
+                    rhs=w_t[:, kc, g * FEAT : (g + 1) * FEAT],
+                    start=(kc == 0),
+                    stop=(kc == K_CHUNKS - 1),
+                )
+                for out, in_, identity in riders[kc * share : (kc + 1) * share]:
+                    nc.tensor.transpose(out, in_, identity)
+            return pl_ps
 
-        def finish_tile(b):
+        def finish_tile(cell, b):
             nc.scalar.activation(out=gate(b, 2), in_=c_new[:, b, :], func=TANH)
-            nc.vector.tensor_tensor(out=h_new[:, b, :], in0=gate(b, 3), in1=gate(b, 2), op=MULT)
+            cell.tensor_tensor(out=h_new[:, b, :], in0=gate(b, 3), in1=gate(b, 2), op=MULT)
             nc.sync.dma_start(out=h_new_view[:, b, :], in_=h_new[:, b, :])
 
-        flip_now(h_flips(0))
-        for block in range(MX_AHEAD):
-            mx_block(block)
-        flip_now(w_flips(0))
+        for q in range(X_AHEAD):
+            x_ps = psum_tp.tile([P, PAIR, 2, P], F32, tag="tp")
+            for out, in_, identity in x_transposes(x_ps, q):
+                nc.tensor.transpose(out, in_, identity)
+            x_copy(x_ps, q)
+        for q in range(X_AHEAD):
+            x_quantise(q)
+        for flip in [h_flip(b) for b in range(PAIR)] + [w_flip(j) for j in range(ROW_TILES)]:
+            flip_ps = psum_tp.tile([P, K_CHUNKS, P], BF16, tag="tp")
+            for out, in_, identity in flip_transposes(flip_ps, flip):
+                nc.tensor.transpose(out, in_, identity)
+            nc.scalar.copy(out=flip[1], in_=flip_ps[:])
+        for g in range(N_GATES):
+            cols = slice(g * FEAT, (g + 1) * FEAT)
+            bias_ps = psum_pl.tile([P, FEAT], F32, tag="pl")
+            nc.tensor.matmul(out=bias_ps[:], lhsT=ones[:], rhs=bias_rows[:, cols], start=True, stop=True)
+            nc.vector.tensor_copy(out=bias_all[:, cols], in_=bias_ps[:])
+        mx_block(0)
 
         for q in range(PAIRS):
+            cell = nc.gpsimd if q + 1 < PAIRS else nc.vector
             for g in range(N_GATES):
                 block = q * N_GATES + g
-                cols = slice(g * FEAT, (g + 1) * FEAT)
-                if block + MX_AHEAD < PAIRS * N_GATES:
-                    mx_block(block + MX_AHEAD)
+                if block + 1 < BLOCKS:
+                    mx_block(block + 1)
                 if q > 0 and g < PAIR:
-                    finish_tile((q - 1) * PAIR + g)
+                    finish_tile(nc.gpsimd, (q - 1) * PAIR + g)
 
-                if q == 0 and g + 1 < N_GATES:
-                    flips = w_flips(g + 1)
-                elif g == N_GATES - 1 and q + 1 < PAIRS:
-                    flips = h_flips(q + 1)
-                else:
-                    flips = []
+                carries_x = g == N_GATES - 1 and q + X_AHEAD < PAIRS
                 sums = []
                 for t in range(PAIR):
-                    b = q * PAIR + t
-                    pl_ps = psum_pl.tile([P, FEAT], F32, tag="pl")
-                    sums.append(pl_ps)
-                    for kc in range(K_CHUNKS):
-                        nc.tensor.matmul(
-                            out=pl_ps[:],
-                            lhsT=h_t[:, kc, b * P : (b + 1) * P],
-                            rhs=w_t[:, kc, cols],
-                            start=(kc == 0),
-                            stop=(kc == K_CHUNKS - 1),
-                        )
-                        rider, half = divmod(t * K_CHUNKS + kc, 2)
-                        if rider < len(flips):
-                            src, dst = flips[rider]
-                            if half == 0:
-                                flip_ps = psum_tp.tile([P, K_CHUNKS, P], BF16, tag="tp")
-                            flip_chunks(flip_ps, src, range(2 * half, 2 * half + 2))
-                            if half == 1:
-                                nc.scalar.copy(out=dst, in_=flip_ps[:])
+                    if q == 0 and g + 1 < N_GATES:
+                        flips = [w_flip((g + 1) * ROW_TILES + t * PAIR + i) for i in range(ROW_TILES // PAIR)]
+                    elif g == N_GATES - 1 and t == 0 and q + 1 < PAIRS:
+                        flips = [h_flip((q + 1) * PAIR + i) for i in range(PAIR)]
+                    else:
+                        flips = []
+                    banks = []
+                    riders = []
+                    for flip in flips:
+                        flip_ps = psum_tp.tile([P, K_CHUNKS, P], BF16, tag="tp")
+                        banks.append(flip_ps)
+                        riders.extend(flip_transposes(flip_ps, flip))
+                    if carries_x and t == 1:
+                        x_ps = psum_tp.tile([P, PAIR, 2, P], F32, tag="tp")
+                        riders = x_transposes(x_ps, q + X_AHEAD)
+                    sums.append(plain_group(q * PAIR + t, g, riders))
+                    for flip, flip_ps in zip(flips, banks):
+                        nc.scalar.copy(out=flip[1], in_=flip_ps[:])
                 for t in range(PAIR):
                     b = q * PAIR + t
                     nc.vector.tensor_tensor(out=gate(b, g), in0=sums[t][:], in1=gate(b, g), op=ADD)
+                if carries_x:
+                    x_copy(x_ps, q + X_AHEAD)
+                    x_quantise(q + X_AHEAD)
                 for t in range(PAIR):
                     b = q * PAIR + t
                     nc.scalar.activation(out=gate(b, g), in_=gate(b, g), func=(TANH if g == 2 else SIGMOID))
@@ -229,8 +247,8 @@ def tile_int8lstmcell_kernel(
                     if g == 1:
                         nc.gpsimd.tensor_tensor(out=gate(b, 1), in0=gate(b, 1), in1=c_sb[:, b, :], op=MULT)
                     if g == 2:
-                        nc.gpsimd.tensor_tensor(out=gate(b, 0), in0=gate(b, 0), in1=gate(b, 2), op=MULT)
-                        nc.gpsimd.tensor_tensor(out=c_new[:, b, :], in0=gate(b, 1), in1=gate(b, 0), op=ADD)
+                        cell.tensor_tensor(out=gate(b, 0), in0=gate(b, 0), in1=gate(b, 2), op=MULT)
+                        cell.tensor_tensor(out=c_new[:, b, :], in0=gate(b, 1), in1=gate(b, 0), op=ADD)
                         nc.sync.dma_start(out=c_new_view[:, b, :], in_=c_new[:, b, :])
         for t in range(PAIR):
-            finish_tile((PAIRS - 1) * PAIR + t)
+            finish_tile(nc.vector, (PAIRS - 1) * PAIR + t)

@@ -25,7 +25,8 @@ PAIR = 2
 PAIRS = TILES // PAIR
 ROW_TILES = FEAT // P
 BLOCKS = PAIRS * N_GATES
-X_AHEAD = 2
+GROUPS = BLOCKS * PAIR
+MX_LEAD = 8
 
 FLOPS = 2 * BATCH * FEAT * GATE_COLS * 2
 
@@ -39,6 +40,7 @@ def tile_int8lstmcell_kernel(
         psum_mx = stack.enter_context(tc.psum_pool(name="psum_mx", bufs=2))
         psum_tp = stack.enter_context(tc.psum_pool(name="psum_tp", bufs=3))
         psum_pl = stack.enter_context(tc.psum_pool(name="psum_pl", bufs=3))
+        stack.enter_context(tc.manual_schedule())
 
         x_view = x.rearrange("(p b) k -> p b k", b=TILES)
         h_view = h_prev.rearrange("(p b) k -> p b k", b=TILES)
@@ -93,27 +95,29 @@ def tile_int8lstmcell_kernel(
                 in_=words_view[:, g * FEAT * 4 : (g + 1) * FEAT * 4].bitcast(I32),
             )
 
-        for q in range(X_AHEAD):
-            load_pair(x_sb, x_view, q)
-        load_pair(h_sb, h_view, 0)
-        load_w_hh(0)
         nc.sync.dma_start(out=bias_rows[0:1, :], in_=bias_ih.rearrange("(o n) -> o n", o=1))
         nc.sync.dma_start(out=bias_rows[1:2, :], in_=bias_hh.rearrange("(o n) -> o n", o=1))
+        load_pair(h_sb, h_view, 0)
+        load_pair(x_sb, x_view, 0)
+        load_w_hh(0)
         for s in range(4):
             nc.sync.dma_start(
                 out=w_plane[32 * s : 32 * s + 4, :].bitcast(I32),
                 in_=w_ih_scales[0, 4 * s : 4 * s + 4, :].bitcast(I32),
             )
         load_words(0)
-        for g in range(1, N_GATES):
+        load_w_hh(1)
+        load_pair(x_sb, x_view, 1)
+        load_words(1)
+        for g in range(2, N_GATES):
             load_w_hh(g)
             load_words(g)
         for q in range(PAIRS):
+            load_pair(c_sb, c_view, q)
             if q + 1 < PAIRS:
                 load_pair(h_sb, h_view, q + 1)
-            load_pair(c_sb, c_view, q)
-            if q + X_AHEAD < PAIRS:
-                load_pair(x_sb, x_view, q + X_AHEAD)
+            if q + 2 < PAIRS:
+                load_pair(x_sb, x_view, q + 2)
 
         grouped_words = x_grouped[:].bitcast(F32).rearrange("p (b r u) -> p b r u", b=TILES, u=2)
 
@@ -125,7 +129,7 @@ def tile_int8lstmcell_kernel(
             ]
 
         def x_copy(x_ps, q):
-            nc.vector.tensor_copy(
+            nc.scalar.copy(
                 out=grouped_words[:, q * PAIR : (q + 1) * PAIR, :, :], in_=x_ps[:].rearrange("p t u r -> p t r u")
             )
 
@@ -137,23 +141,23 @@ def tile_int8lstmcell_kernel(
                 in_=x_grouped[:, q * PAIR * P * 4 : (q + 1) * PAIR * P * 4],
             )
 
-        def mx_block(block):
+        def mx_pass(group):
+            block, t = divmod(group, PAIR)
             q, g = divmod(block, N_GATES)
+            b = q * PAIR + t
+            rows = slice(b * P, (b + 1) * P)
             cols = slice(g * FEAT, (g + 1) * FEAT)
-            for t in range(PAIR):
-                b = q * PAIR + t
-                rows = slice(b * P, (b + 1) * P)
-                mx_ps = psum_mx.tile([P, FEAT], F32, tag="mx")
-                nc.tensor.matmul_mx(
-                    out=mx_ps[:],
-                    lhsT=x_codes[:, rows].bitcast(FP8X4),
-                    lhsT_scale=x_plane[:, rows],
-                    rhs=w_words[:, cols].bitcast(FP8X4),
-                    rhs_scale=w_plane[:, cols],
-                    start=True,
-                    stop=True,
-                )
-                nc.vector.tensor_tensor(out=gate(b, g), in0=mx_ps[:], in1=bias_all[:, cols], op=ADD)
+            mx_ps = psum_mx.tile([P, FEAT], F32, tag="mx")
+            nc.tensor.matmul_mx(
+                out=mx_ps[:],
+                lhsT=x_codes[:, rows].bitcast(FP8X4),
+                lhsT_scale=x_plane[:, rows],
+                rhs=w_words[:, cols].bitcast(FP8X4),
+                rhs_scale=w_plane[:, cols],
+                start=True,
+                stop=True,
+            )
+            nc.vector.tensor_tensor(out=gate(b, g), in0=mx_ps[:], in1=bias_all[:, cols], op=ADD)
 
         def w_flip(j):
             return (w_sb[:, j, :], w_t[:, :, j * P : (j + 1) * P])
@@ -184,40 +188,41 @@ def tile_int8lstmcell_kernel(
             cell.tensor_tensor(out=h_new[:, b, :], in0=gate(b, 3), in1=gate(b, 2), op=MULT)
             nc.sync.dma_start(out=h_new_view[:, b, :], in_=h_new[:, b, :])
 
-        for q in range(X_AHEAD):
-            x_ps = psum_tp.tile([P, PAIR, 2, P], F32, tag="tp")
-            for out, in_, identity in x_transposes(x_ps, q):
-                nc.tensor.transpose(out, in_, identity)
-            x_copy(x_ps, q)
-        for q in range(X_AHEAD):
-            x_quantise(q)
-        for flip in [h_flip(b) for b in range(PAIR)] + [w_flip(j) for j in range(ROW_TILES)]:
-            flip_ps = psum_tp.tile([P, K_CHUNKS, P], BF16, tag="tp")
-            for out, in_, identity in flip_transposes(flip_ps, flip):
-                nc.tensor.transpose(out, in_, identity)
-            nc.scalar.copy(out=flip[1], in_=flip_ps[:])
+        first_flips = [h_flip(b) for b in range(PAIR)] + [w_flip(j) for j in range(ROW_TILES)]
         for g in range(N_GATES):
             cols = slice(g * FEAT, (g + 1) * FEAT)
             bias_ps = psum_pl.tile([P, FEAT], F32, tag="pl")
             nc.tensor.matmul(out=bias_ps[:], lhsT=ones[:], rhs=bias_rows[:, cols], start=True, stop=True)
             nc.vector.tensor_copy(out=bias_all[:, cols], in_=bias_ps[:])
-        mx_block(0)
+            if g == 1:
+                x_ps = psum_tp.tile([P, PAIR, 2, P], F32, tag="tp")
+                for out, in_, identity in x_transposes(x_ps, 0):
+                    nc.tensor.transpose(out, in_, identity)
+                x_copy(x_ps, 0)
+            else:
+                for flip in first_flips[:PAIR]:
+                    flip_ps = psum_tp.tile([P, K_CHUNKS, P], BF16, tag="tp")
+                    for out, in_, identity in flip_transposes(flip_ps, flip):
+                        nc.tensor.transpose(out, in_, identity)
+                    nc.scalar.copy(out=flip[1], in_=flip_ps[:])
+                first_flips = first_flips[PAIR:]
+        x_quantise(0)
 
+        mx_done = 0
         for q in range(PAIRS):
             cell = nc.gpsimd if q + 1 < PAIRS else nc.vector
             for g in range(N_GATES):
                 block = q * N_GATES + g
-                if block + 1 < BLOCKS:
-                    mx_block(block + 1)
                 if q > 0 and g < PAIR:
                     finish_tile(nc.gpsimd, (q - 1) * PAIR + g)
 
-                carries_x = g == N_GATES - 1 and q + X_AHEAD < PAIRS
-                sums = []
+                last_of_pair = g == N_GATES - 1 and q + 1 < PAIRS
+                x_pair = 1 if block == 0 else q + 2
+                carries_x = block == 0 or (g == 2 and q + 2 < PAIRS)
                 for t in range(PAIR):
                     if q == 0 and g + 1 < N_GATES:
                         flips = [w_flip((g + 1) * ROW_TILES + t * PAIR + i) for i in range(ROW_TILES // PAIR)]
-                    elif g == N_GATES - 1 and t == 0 and q + 1 < PAIRS:
+                    elif last_of_pair and t == 0:
                         flips = [h_flip((q + 1) * PAIR + i) for i in range(PAIR)]
                     else:
                         flips = []
@@ -229,16 +234,20 @@ def tile_int8lstmcell_kernel(
                         riders.extend(flip_transposes(flip_ps, flip))
                     if carries_x and t == 1:
                         x_ps = psum_tp.tile([P, PAIR, 2, P], F32, tag="tp")
-                        riders = x_transposes(x_ps, q + X_AHEAD)
-                    sums.append(plain_group(q * PAIR + t, g, riders))
+                        riders.extend(x_transposes(x_ps, x_pair))
+                    b = q * PAIR + t
+                    pl_ps = plain_group(b, g, riders)
                     for flip, flip_ps in zip(flips, banks):
                         nc.scalar.copy(out=flip[1], in_=flip_ps[:])
-                for t in range(PAIR):
-                    b = q * PAIR + t
-                    nc.vector.tensor_tensor(out=gate(b, g), in0=sums[t][:], in1=gate(b, g), op=ADD)
+                    group = block * PAIR + t
+                    mx_wanted = min(GROUPS, group + 1 + min(group + 1, MX_LEAD))
+                    for mx in range(mx_done, mx_wanted):
+                        mx_pass(mx)
+                    mx_done = mx_wanted
+                    nc.vector.tensor_tensor(out=gate(b, g), in0=pl_ps[:], in1=gate(b, g), op=ADD)
                 if carries_x:
-                    x_copy(x_ps, q + X_AHEAD)
-                    x_quantise(q + X_AHEAD)
+                    x_copy(x_ps, x_pair)
+                    x_quantise(x_pair)
                 for t in range(PAIR):
                     b = q * PAIR + t
                     nc.scalar.activation(out=gate(b, g), in_=gate(b, g), func=(TANH if g == 2 else SIGMOID))

@@ -78,8 +78,8 @@ def tile_int8lstmcell_kernel(
         nc.vector.memset(w_plane[:].bitcast(I32), 0)
         nc.vector.memset(ones[:], 1.0)
         nc.vector.memset(warm[:], 0.0)
-        make_identity(nc, ident_f32[:])
         make_identity(nc, ident_bf[:])
+        make_identity(nc, ident_f32[:])
         nc.scalar.activation(out=warm[:], in_=warm[:], func=SIGMOID)
 
         def load_pair(dst, src, q):
@@ -95,10 +95,10 @@ def tile_int8lstmcell_kernel(
                 in_=words_view[:, g * FEAT * 4 : (g + 1) * FEAT * 4].bitcast(I32),
             )
 
-        nc.sync.dma_start(out=bias_rows[0:1, :], in_=bias_ih.rearrange("(o n) -> o n", o=1))
-        nc.sync.dma_start(out=bias_rows[1:2, :], in_=bias_hh.rearrange("(o n) -> o n", o=1))
         load_pair(h_sb, h_view, 0)
         load_pair(x_sb, x_view, 0)
+        nc.sync.dma_start(out=bias_rows[0:1, :], in_=bias_ih.rearrange("(o n) -> o n", o=1))
+        nc.sync.dma_start(out=bias_rows[1:2, :], in_=bias_hh.rearrange("(o n) -> o n", o=1))
         load_w_hh(0)
         for s in range(4):
             nc.sync.dma_start(
@@ -169,7 +169,7 @@ def tile_int8lstmcell_kernel(
             return [(flip_ps[:, kc, :], flip[0][:, kc * P : (kc + 1) * P], ident_bf[:]) for kc in range(K_CHUNKS)]
 
         def plain_group(b, g, riders):
-            share = len(riders) // K_CHUNKS
+            share = -(-len(riders) // (K_CHUNKS - 1))
             pl_ps = psum_pl.tile([P, FEAT], F32, tag="pl")
             for kc in range(K_CHUNKS):
                 nc.tensor.matmul(
@@ -183,17 +183,23 @@ def tile_int8lstmcell_kernel(
                     nc.tensor.transpose(out, in_, identity)
             return pl_ps
 
-        def finish_tile(cell, b):
+        def activate(b, g):
+            nc.scalar.activation(out=gate(b, g), in_=gate(b, g), func=(TANH if g == 2 else SIGMOID))
+
+        def c_sum(cell, b):
+            cell.tensor_tensor(out=gate(b, 0), in0=gate(b, 0), in1=gate(b, 2), op=MULT)
+            cell.tensor_tensor(out=c_new[:, b, :], in0=gate(b, 1), in1=gate(b, 0), op=ADD)
+            nc.sync.dma_start(out=c_new_view[:, b, :], in_=c_new[:, b, :])
+
+        def tanh_c_new(b):
             nc.scalar.activation(out=gate(b, 2), in_=c_new[:, b, :], func=TANH)
+
+        def h_product(cell, b):
             cell.tensor_tensor(out=h_new[:, b, :], in0=gate(b, 3), in1=gate(b, 2), op=MULT)
             nc.sync.dma_start(out=h_new_view[:, b, :], in_=h_new[:, b, :])
 
         first_flips = [h_flip(b) for b in range(PAIR)] + [w_flip(j) for j in range(ROW_TILES)]
         for g in range(N_GATES):
-            cols = slice(g * FEAT, (g + 1) * FEAT)
-            bias_ps = psum_pl.tile([P, FEAT], F32, tag="pl")
-            nc.tensor.matmul(out=bias_ps[:], lhsT=ones[:], rhs=bias_rows[:, cols], start=True, stop=True)
-            nc.vector.tensor_copy(out=bias_all[:, cols], in_=bias_ps[:])
             if g == 1:
                 x_ps = psum_tp.tile([P, PAIR, 2, P], F32, tag="tp")
                 for out, in_, identity in x_transposes(x_ps, 0):
@@ -206,15 +212,21 @@ def tile_int8lstmcell_kernel(
                         nc.tensor.transpose(out, in_, identity)
                     nc.scalar.copy(out=flip[1], in_=flip_ps[:])
                 first_flips = first_flips[PAIR:]
+            cols = slice(g * FEAT, (g + 1) * FEAT)
+            bias_ps = psum_pl.tile([P, FEAT], F32, tag="pl")
+            nc.tensor.matmul(out=bias_ps[:], lhsT=ones[:], rhs=bias_rows[:, cols], start=True, stop=True)
+            nc.vector.tensor_copy(out=bias_all[:, cols], in_=bias_ps[:])
         x_quantise(0)
 
         mx_done = 0
         for q in range(PAIRS):
-            cell = nc.gpsimd if q + 1 < PAIRS else nc.vector
+            last_pair = q == PAIRS - 1
+            cell = nc.vector if last_pair else nc.gpsimd
             for g in range(N_GATES):
                 block = q * N_GATES + g
                 if q > 0 and g < PAIR:
-                    finish_tile(nc.gpsimd, (q - 1) * PAIR + g)
+                    tanh_c_new((q - 1) * PAIR + g)
+                    h_product(nc.gpsimd, (q - 1) * PAIR + g)
 
                 last_of_pair = g == N_GATES - 1 and q + 1 < PAIRS
                 x_pair = 1 if block == 0 else q + 2
@@ -244,20 +256,21 @@ def tile_int8lstmcell_kernel(
                     for mx in range(mx_done, mx_wanted):
                         mx_pass(mx)
                     mx_done = mx_wanted
+                    if g == N_GATES - 1:
+                        c_sum(cell, b)
+                        if last_pair:
+                            tanh_c_new(b)
                     nc.vector.tensor_tensor(out=gate(b, g), in0=pl_ps[:], in1=gate(b, g), op=ADD)
+                    if g == N_GATES - 1:
+                        activate(b, g)
                 if carries_x:
                     x_copy(x_ps, x_pair)
                     x_quantise(x_pair)
                 for t in range(PAIR):
                     b = q * PAIR + t
-                    nc.scalar.activation(out=gate(b, g), in_=gate(b, g), func=(TANH if g == 2 else SIGMOID))
-                for t in range(PAIR):
-                    b = q * PAIR + t
+                    if g < N_GATES - 1:
+                        activate(b, g)
                     if g == 1:
                         nc.gpsimd.tensor_tensor(out=gate(b, 1), in0=gate(b, 1), in1=c_sb[:, b, :], op=MULT)
-                    if g == 2:
-                        cell.tensor_tensor(out=gate(b, 0), in0=gate(b, 0), in1=gate(b, 2), op=MULT)
-                        cell.tensor_tensor(out=c_new[:, b, :], in0=gate(b, 1), in1=gate(b, 0), op=ADD)
-                        nc.sync.dma_start(out=c_new_view[:, b, :], in_=c_new[:, b, :])
         for t in range(PAIR):
-            finish_tile(nc.vector, (PAIRS - 1) * PAIR + t)
+            h_product(nc.vector, (PAIRS - 1) * PAIR + t)

@@ -21,6 +21,7 @@ N_GATES = 4
 GATE_COLS = N_GATES * FEAT
 TILES = BATCH // P
 K_CHUNKS = FEAT // P
+WORD_CHUNKS = FEAT // 2 // P
 PAIR = 2
 PAIRS = TILES // PAIR
 ROW_TILES = FEAT // P
@@ -59,14 +60,15 @@ def tile_int8lstmcell_kernel(
         bias_rows = keep.tile([P, GATE_COLS], BF16)
         bias_all = keep.tile([P, GATE_COLS], F32)
         ones = keep.tile([P, P], BF16)
-        ident_bf = keep.tile([P, P], BF16)
         ident_f32 = keep.tile([P, P], F32)
         warm = keep.tile([P, 1], F32)
         x_grouped = keep.tile([P, BATCH * 4], BF16, align_bytes=64)
         x_codes = keep.tile([P, BATCH], U32, align_bytes=64)
         x_plane = keep.tile([P, BATCH], U8, align_bytes=64)
-        h_t = keep.tile([P, K_CHUNKS, BATCH], BF16)
-        w_t = keep.tile([P, K_CHUNKS, GATE_COLS], BF16)
+        h_t = keep.tile([P, WORD_CHUNKS, BATCH], F32)
+        w_t = keep.tile([P, WORD_CHUNKS, GATE_COLS], F32)
+        h_t_halves = h_t[:].rearrange("p j r -> p (j r)").bitcast(BF16).rearrange("p (j r e) -> p j r e", j=WORD_CHUNKS, e=2)
+        w_t_halves = w_t[:].rearrange("p j r -> p (j r)").bitcast(BF16).rearrange("p (j r e) -> p j r e", j=WORD_CHUNKS, e=2)
         gates = keep.tile([P, TILES, GATE_COLS], F32)
         c_new = keep.tile([P, TILES, FEAT], F32)
         h_new = keep.tile([P, TILES, FEAT], F32)
@@ -78,7 +80,6 @@ def tile_int8lstmcell_kernel(
         nc.vector.memset(w_plane[:].bitcast(I32), 0)
         nc.vector.memset(ones[:], 1.0)
         nc.vector.memset(warm[:], 0.0)
-        make_identity(nc, ident_bf[:])
         make_identity(nc, ident_f32[:])
         nc.scalar.activation(out=warm[:], in_=warm[:], func=SIGMOID)
 
@@ -159,14 +160,21 @@ def tile_int8lstmcell_kernel(
             )
             nc.vector.tensor_tensor(out=gate(b, g), in0=mx_ps[:], in1=bias_all[:, cols], op=ADD)
 
-        def w_flip(j):
-            return (w_sb[:, j, :], w_t[:, :, j * P : (j + 1) * P])
+        def w_flip(jj):
+            return ([w_sb[:, jj * PAIR + i, :] for i in range(PAIR)], w_t[:, :, jj * PAIR * P : (jj + 1) * PAIR * P])
 
-        def h_flip(b):
-            return (h_sb[:, b, :], h_t[:, :, b * P : (b + 1) * P])
+        def h_flip(q):
+            return ([h_sb[:, q * PAIR + i, :] for i in range(PAIR)], h_t[:, :, q * PAIR * P : (q + 1) * PAIR * P])
 
         def flip_transposes(flip_ps, flip):
-            return [(flip_ps[:, kc, :], flip[0][:, kc * P : (kc + 1) * P], ident_bf[:]) for kc in range(K_CHUNKS)]
+            return [
+                (flip_ps[:, j, i, :], flip[0][i].bitcast(F32)[:, j * P : (j + 1) * P], ident_f32[:])
+                for i in range(PAIR)
+                for j in range(WORD_CHUNKS)
+            ]
+
+        def flip_copy(flip_ps, flip):
+            nc.scalar.copy(out=flip[1], in_=flip_ps[:].rearrange("p j i r -> p j (i r)"))
 
         def plain_group(b, g, riders):
             share = -(-len(riders) // (K_CHUNKS - 1))
@@ -174,8 +182,8 @@ def tile_int8lstmcell_kernel(
             for kc in range(K_CHUNKS):
                 nc.tensor.matmul(
                     out=pl_ps[:],
-                    lhsT=h_t[:, kc, b * P : (b + 1) * P],
-                    rhs=w_t[:, kc, g * FEAT : (g + 1) * FEAT],
+                    lhsT=h_t_halves[:, kc // 2, b * P : (b + 1) * P, kc % 2],
+                    rhs=w_t_halves[:, kc // 2, g * FEAT : (g + 1) * FEAT, kc % 2],
                     start=(kc == 0),
                     stop=(kc == K_CHUNKS - 1),
                 )
@@ -198,7 +206,7 @@ def tile_int8lstmcell_kernel(
             cell.tensor_tensor(out=h_new[:, b, :], in0=gate(b, 3), in1=gate(b, 2), op=MULT)
             nc.sync.dma_start(out=h_new_view[:, b, :], in_=h_new[:, b, :])
 
-        first_flips = [h_flip(b) for b in range(PAIR)] + [w_flip(j) for j in range(ROW_TILES)]
+        first_flips = [h_flip(0)] + [w_flip(jj) for jj in range(ROW_TILES // PAIR)]
         for g in range(N_GATES):
             if g == 1:
                 x_ps = psum_tp.tile([P, PAIR, 2, P], F32, tag="tp")
@@ -206,12 +214,12 @@ def tile_int8lstmcell_kernel(
                     nc.tensor.transpose(out, in_, identity)
                 x_copy(x_ps, 0)
             else:
-                for flip in first_flips[:PAIR]:
-                    flip_ps = psum_tp.tile([P, K_CHUNKS, P], BF16, tag="tp")
-                    for out, in_, identity in flip_transposes(flip_ps, flip):
-                        nc.tensor.transpose(out, in_, identity)
-                    nc.scalar.copy(out=flip[1], in_=flip_ps[:])
-                first_flips = first_flips[PAIR:]
+                flip = first_flips[0]
+                flip_ps = psum_tp.tile([P, WORD_CHUNKS, PAIR, P], F32, tag="tp")
+                for out, in_, identity in flip_transposes(flip_ps, flip):
+                    nc.tensor.transpose(out, in_, identity)
+                flip_copy(flip_ps, flip)
+                first_flips = first_flips[1:]
             cols = slice(g * FEAT, (g + 1) * FEAT)
             bias_ps = psum_pl.tile([P, FEAT], F32, tag="pl")
             nc.tensor.matmul(out=bias_ps[:], lhsT=ones[:], rhs=bias_rows[:, cols], start=True, stop=True)
@@ -233,15 +241,15 @@ def tile_int8lstmcell_kernel(
                 carries_x = block == 0 or (g == 2 and q + 2 < PAIRS)
                 for t in range(PAIR):
                     if q == 0 and g + 1 < N_GATES:
-                        flips = [w_flip((g + 1) * ROW_TILES + t * PAIR + i) for i in range(ROW_TILES // PAIR)]
+                        flips = [w_flip((g + 1) * (ROW_TILES // PAIR) + t)]
                     elif last_of_pair and t == 0:
-                        flips = [h_flip((q + 1) * PAIR + i) for i in range(PAIR)]
+                        flips = [h_flip(q + 1)]
                     else:
                         flips = []
                     banks = []
                     riders = []
                     for flip in flips:
-                        flip_ps = psum_tp.tile([P, K_CHUNKS, P], BF16, tag="tp")
+                        flip_ps = psum_tp.tile([P, WORD_CHUNKS, PAIR, P], F32, tag="tp")
                         banks.append(flip_ps)
                         riders.extend(flip_transposes(flip_ps, flip))
                     if carries_x and t == 1:
@@ -250,7 +258,7 @@ def tile_int8lstmcell_kernel(
                     b = q * PAIR + t
                     pl_ps = plain_group(b, g, riders)
                     for flip, flip_ps in zip(flips, banks):
-                        nc.scalar.copy(out=flip[1], in_=flip_ps[:])
+                        flip_copy(flip_ps, flip)
                     group = block * PAIR + t
                     mx_wanted = min(GROUPS, group + 1 + min(group + 1, MX_LEAD))
                     for mx in range(mx_done, mx_wanted):

@@ -38,9 +38,7 @@ def tile_int8lstmcell_kernel(
     nc = tc.nc
     with ExitStack() as stack:
         keep = stack.enter_context(tc.tile_pool(name="keep", bufs=1))
-        psum_mx = stack.enter_context(tc.psum_pool(name="psum_mx", bufs=2))
-        psum_tp = stack.enter_context(tc.psum_pool(name="psum_tp", bufs=3))
-        psum_pl = stack.enter_context(tc.psum_pool(name="psum_pl", bufs=3))
+        psum = stack.enter_context(tc.psum_pool(name="psum", bufs=8))
         stack.enter_context(tc.manual_schedule())
 
         x_view = x.rearrange("(p b) k -> p b k", b=TILES)
@@ -86,8 +84,8 @@ def tile_int8lstmcell_kernel(
         def load_pair(dst, src, q):
             nc.sync.dma_start(out=dst[:, q * PAIR : (q + 1) * PAIR, :], in_=src[:, q * PAIR : (q + 1) * PAIR, :])
 
-        def load_w_hh(g):
-            row_tiles = slice(g * ROW_TILES, (g + 1) * ROW_TILES)
+        def load_w_hh(jj):
+            row_tiles = slice(jj * PAIR, (jj + 1) * PAIR)
             nc.sync.dma_start(out=w_sb[:, row_tiles, :], in_=w_hh_view[:, row_tiles, :])
 
         def load_words(g):
@@ -97,22 +95,27 @@ def tile_int8lstmcell_kernel(
             )
 
         load_pair(h_sb, h_view, 0)
-        load_pair(x_sb, x_view, 0)
         nc.sync.dma_start(out=bias_rows[0:1, :], in_=bias_ih.rearrange("(o n) -> o n", o=1))
         nc.sync.dma_start(out=bias_rows[1:2, :], in_=bias_hh.rearrange("(o n) -> o n", o=1))
         load_w_hh(0)
+        load_w_hh(1)
+        load_w_hh(2)
+        load_pair(x_sb, x_view, 0)
+        load_w_hh(3)
         for s in range(4):
             nc.sync.dma_start(
                 out=w_plane[32 * s : 32 * s + 4, :].bitcast(I32),
                 in_=w_ih_scales[0, 4 * s : 4 * s + 4, :].bitcast(I32),
             )
         load_words(0)
-        load_w_hh(1)
-        load_pair(x_sb, x_view, 1)
         load_words(1)
-        for g in range(2, N_GATES):
-            load_w_hh(g)
-            load_words(g)
+        load_w_hh(4)
+        load_pair(x_sb, x_view, 1)
+        load_w_hh(5)
+        load_words(2)
+        load_w_hh(6)
+        load_w_hh(7)
+        load_words(3)
         for q in range(PAIRS):
             load_pair(c_sb, c_view, q)
             if q + 1 < PAIRS:
@@ -142,13 +145,10 @@ def tile_int8lstmcell_kernel(
                 in_=x_grouped[:, q * PAIR * P * 4 : (q + 1) * PAIR * P * 4],
             )
 
-        def mx_pass(group):
-            block, t = divmod(group, PAIR)
-            q, g = divmod(block, N_GATES)
-            b = q * PAIR + t
+        def mx_pass(b, g):
             rows = slice(b * P, (b + 1) * P)
             cols = slice(g * FEAT, (g + 1) * FEAT)
-            mx_ps = psum_mx.tile([P, FEAT], F32, tag="mx")
+            mx_ps = psum.tile([P, FEAT], F32, tag="bank")
             nc.tensor.matmul_mx(
                 out=mx_ps[:],
                 lhsT=x_codes[:, rows].bitcast(FP8X4),
@@ -158,7 +158,16 @@ def tile_int8lstmcell_kernel(
                 start=True,
                 stop=True,
             )
-            nc.vector.tensor_tensor(out=gate(b, g), in0=mx_ps[:], in1=bias_all[:, cols], op=ADD)
+            return mx_ps
+
+        begun = set()
+
+        def fetch(sums_ps, b, g):
+            complete = (b, g) in begun
+            other = gate(b, g) if complete else bias_all[:, g * FEAT : (g + 1) * FEAT]
+            nc.vector.tensor_tensor(out=gate(b, g), in0=sums_ps[:], in1=other, op=ADD)
+            begun.add((b, g))
+            return complete
 
         def w_flip(jj):
             return ([w_sb[:, jj * PAIR + i, :] for i in range(PAIR)], w_t[:, :, jj * PAIR * P : (jj + 1) * PAIR * P])
@@ -176,26 +185,34 @@ def tile_int8lstmcell_kernel(
         def flip_copy(flip_ps, flip):
             nc.scalar.copy(out=flip[1], in_=flip_ps[:].rearrange("p j i r -> p j (i r)"))
 
-        def plain_group(b, g, riders):
+        def plain_matmuls(pl_ps, b, g, lo, hi, riders):
             share = -(-len(riders) // (K_CHUNKS - 1))
-            pl_ps = psum_pl.tile([P, FEAT], F32, tag="pl")
             for kc in range(K_CHUNKS):
                 nc.tensor.matmul(
-                    out=pl_ps[:],
+                    out=pl_ps[:, lo:hi],
                     lhsT=h_t_halves[:, kc // 2, b * P : (b + 1) * P, kc % 2],
-                    rhs=w_t_halves[:, kc // 2, g * FEAT : (g + 1) * FEAT, kc % 2],
+                    rhs=w_t_halves[:, kc // 2, g * FEAT + lo : g * FEAT + hi, kc % 2],
                     start=(kc == 0),
                     stop=(kc == K_CHUNKS - 1),
                 )
                 for out, in_, identity in riders[kc * share : (kc + 1) * share]:
                     nc.tensor.transpose(out, in_, identity)
+
+        def plain_group(b, g, riders):
+            pl_ps = psum.tile([P, FEAT], F32, tag="bank")
+            plain_matmuls(pl_ps, b, g, 0, FEAT, riders)
             return pl_ps
 
         def activate(b, g):
             nc.scalar.activation(out=gate(b, g), in_=gate(b, g), func=(TANH if g == 2 else SIGMOID))
 
-        def c_sum(cell, b):
+        def f_times_c(cell, b):
+            cell.tensor_tensor(out=gate(b, 1), in0=gate(b, 1), in1=c_sb[:, b, :], op=MULT)
+
+        def i_times_g(cell, b):
             cell.tensor_tensor(out=gate(b, 0), in0=gate(b, 0), in1=gate(b, 2), op=MULT)
+
+        def c_sum(cell, b):
             cell.tensor_tensor(out=c_new[:, b, :], in0=gate(b, 1), in1=gate(b, 0), op=ADD)
             nc.sync.dma_start(out=c_new_view[:, b, :], in_=c_new[:, b, :])
 
@@ -206,79 +223,122 @@ def tile_int8lstmcell_kernel(
             cell.tensor_tensor(out=h_new[:, b, :], in0=gate(b, 3), in1=gate(b, 2), op=MULT)
             nc.sync.dma_start(out=h_new_view[:, b, :], in_=h_new[:, b, :])
 
-        first_flips = [h_flip(0)] + [w_flip(jj) for jj in range(ROW_TILES // PAIR)]
-        for g in range(N_GATES):
-            if g == 1:
-                x_ps = psum_tp.tile([P, PAIR, 2, P], F32, tag="tp")
-                for out, in_, identity in x_transposes(x_ps, 0):
-                    nc.tensor.transpose(out, in_, identity)
-                x_copy(x_ps, 0)
-            else:
-                flip = first_flips[0]
-                flip_ps = psum_tp.tile([P, WORD_CHUNKS, PAIR, P], F32, tag="tp")
-                for out, in_, identity in flip_transposes(flip_ps, flip):
-                    nc.tensor.transpose(out, in_, identity)
-                flip_copy(flip_ps, flip)
-                first_flips = first_flips[1:]
+        def flip_now(flip):
+            flip_ps = psum.tile([P, WORD_CHUNKS, PAIR, P], F32, tag="bank")
+            for out, in_, identity in flip_transposes(flip_ps, flip):
+                nc.tensor.transpose(out, in_, identity)
+            flip_copy(flip_ps, flip)
+
+        def spread_biases(g, copy):
             cols = slice(g * FEAT, (g + 1) * FEAT)
-            bias_ps = psum_pl.tile([P, FEAT], F32, tag="pl")
+            bias_ps = psum.tile([P, FEAT], F32, tag="bank")
             nc.tensor.matmul(out=bias_ps[:], lhsT=ones[:], rhs=bias_rows[:, cols], start=True, stop=True)
-            nc.vector.tensor_copy(out=bias_all[:, cols], in_=bias_ps[:])
-        x_quantise(0)
+            copy(out=bias_all[:, cols], in_=bias_ps[:])
 
-        mx_done = 0
+        flip_now(h_flip(0))
+        flip_now(w_flip(0))
+        spread_biases(0, nc.vector.tensor_copy)
+        flip_now(w_flip(1))
+
+        block_order = []
         for q in range(PAIRS):
-            last_pair = q == PAIRS - 1
-            cell = nc.vector if last_pair else nc.gpsimd
-            for g in range(N_GATES):
-                block = q * N_GATES + g
-                if q > 0 and g < PAIR:
-                    tanh_c_new((q - 1) * PAIR + g)
-                    h_product(nc.gpsimd, (q - 1) * PAIR + g)
+            block_order.extend([(q, g) for g in range(N_GATES - 1)])
+            if q > 0:
+                block_order.append((q - 1, N_GATES - 1))
+        block_order.append((PAIRS - 1, N_GATES - 1))
+        groups = [(q * PAIR + t, g) for q, g in block_order for t in range(PAIR)]
 
-                last_of_pair = g == N_GATES - 1 and q + 1 < PAIRS
-                x_pair = 1 if block == 0 else q + 2
-                carries_x = block == 0 or (g == 2 and q + 2 < PAIRS)
-                for t in range(PAIR):
-                    if q == 0 and g + 1 < N_GATES:
-                        flips = [w_flip((g + 1) * (ROW_TILES // PAIR) + t)]
-                    elif last_of_pair and t == 0:
-                        flips = [h_flip(q + 1)]
-                    else:
-                        flips = []
-                    banks = []
-                    riders = []
-                    for flip in flips:
-                        flip_ps = psum_tp.tile([P, WORD_CHUNKS, PAIR, P], F32, tag="tp")
-                        banks.append(flip_ps)
-                        riders.extend(flip_transposes(flip_ps, flip))
-                    if carries_x and t == 1:
-                        x_ps = psum_tp.tile([P, PAIR, 2, P], F32, tag="tp")
-                        riders.extend(x_transposes(x_ps, x_pair))
-                    b = q * PAIR + t
-                    pl_ps = plain_group(b, g, riders)
-                    for flip, flip_ps in zip(flips, banks):
-                        flip_copy(flip_ps, flip)
-                    group = block * PAIR + t
-                    mx_wanted = min(GROUPS, group + 1 + min(group + 1, MX_LEAD))
-                    for mx in range(mx_done, mx_wanted):
-                        mx_pass(mx)
-                    mx_done = mx_wanted
-                    if g == N_GATES - 1:
-                        c_sum(cell, b)
-                        if last_pair:
-                            tanh_c_new(b)
-                    nc.vector.tensor_tensor(out=gate(b, g), in0=pl_ps[:], in1=gate(b, g), op=ADD)
-                    if g == N_GATES - 1:
-                        activate(b, g)
-                if carries_x:
-                    x_copy(x_ps, x_pair)
-                    x_quantise(x_pair)
-                for t in range(PAIR):
-                    b = q * PAIR + t
-                    if g < N_GATES - 1:
-                        activate(b, g)
-                    if g == 1:
-                        nc.gpsimd.tensor_tensor(out=gate(b, 1), in0=gate(b, 1), in1=c_sb[:, b, :], op=MULT)
-        for t in range(PAIR):
-            h_product(nc.vector, (PAIRS - 1) * PAIR + t)
+        later = {}
+
+        def at_slot(s, call):
+            later.setdefault(s, []).append(call)
+
+        def finish_gate(s, b, g):
+            activate(b, g)
+            last_pair = b // PAIR == PAIRS - 1
+            last_tile = b == TILES - 1
+            if g == 1:
+                f_times_c(nc.gpsimd, b)
+            elif g == 2:
+                if last_tile:
+                    at_slot(s + 1, lambda: i_times_g(nc.vector, b))
+                    at_slot(s + 2, lambda: c_sum(nc.vector, b))
+                    at_slot(s + 2, lambda: tanh_c_new(b))
+                else:
+                    i_times_g(nc.gpsimd, b)
+                    c_sum(nc.gpsimd, b)
+                    at_slot(s + (2 if last_pair else 4), lambda: tanh_c_new(b))
+            elif g == 3:
+                if last_pair:
+                    at_slot(GROUPS - 1, lambda: h_product(nc.vector, b))
+                else:
+                    h_product(nc.gpsimd, b)
+
+        half = FEAT // 2
+        pl_0 = psum.tile([P, FEAT], F32, tag="bank")
+        pl_1 = psum.tile([P, FEAT], F32, tag="bank")
+        f_ps_0 = psum.tile([P, WORD_CHUNKS, PAIR, P], F32, tag="bank")
+        plain_matmuls(pl_0, 0, 0, 0, half, flip_transposes(f_ps_0, w_flip(2)))
+        flip_copy(f_ps_0, w_flip(2))
+        x_ps = psum.tile([P, PAIR, 2, P], F32, tag="bank")
+        plain_matmuls(pl_1, 1, 0, 0, half, x_transposes(x_ps, 0))
+        x_copy(x_ps, 0)
+        f_ps_1 = psum.tile([P, WORD_CHUNKS, PAIR, P], F32, tag="bank")
+        plain_matmuls(pl_0, 0, 0, half, FEAT, flip_transposes(f_ps_1, w_flip(3)))
+        flip_copy(f_ps_1, w_flip(3))
+        plain_matmuls(pl_1, 1, 0, half, FEAT, [])
+        for g in range(1, N_GATES):
+            spread_biases(g, nc.scalar.copy)
+        x_quantise(0)
+        mx_done = 2 * PAIR
+        fetch(pl_0, 0, 0)
+        fetch(pl_1, 1, 0)
+        passes = [(mx_pass(mb, mg), mb, mg) for mb, mg in groups[:mx_done]]
+        for mx_ps, mb, mg in passes:
+            if fetch(mx_ps, mb, mg):
+                finish_gate(1, mb, mg)
+
+        for s, (b, g) in enumerate(groups):
+            if s < PAIR:
+                continue
+            q, t = divmod(b, PAIR)
+            if q == 0 and g == 1:
+                flips = [w_flip((g + 1) * (ROW_TILES // PAIR) + t)]
+            elif q == 1 and g == 0:
+                flips = [w_flip(3 * (ROW_TILES // PAIR) + t)]
+            elif g == 2 and t == 0 and q + 1 < PAIRS:
+                flips = [h_flip(q + 1)]
+            else:
+                flips = []
+            if s == PAIR:
+                x_pair = 1
+            elif g == 2 and t == 1 and q + 2 < PAIRS:
+                x_pair = q + 2
+            else:
+                x_pair = 0
+            banks = []
+            riders = []
+            for flip in flips:
+                flip_ps = psum.tile([P, WORD_CHUNKS, PAIR, P], F32, tag="bank")
+                banks.append(flip_ps)
+                riders.extend(flip_transposes(flip_ps, flip))
+            if x_pair:
+                x_ps = psum.tile([P, PAIR, 2, P], F32, tag="bank")
+                riders.extend(x_transposes(x_ps, x_pair))
+            pl_ps = plain_group(b, g, riders)
+            for flip, flip_ps in zip(flips, banks):
+                flip_copy(flip_ps, flip)
+            if x_pair:
+                x_copy(x_ps, x_pair)
+            mx_wanted = min(GROUPS, s + 1 + min(s + 1, MX_LEAD))
+            passes = [(mx_pass(mb, mg), mb, mg) for mb, mg in groups[mx_done:mx_wanted]]
+            mx_done = mx_wanted
+            if fetch(pl_ps, b, g):
+                finish_gate(s, b, g)
+            for mx_ps, mb, mg in passes:
+                if fetch(mx_ps, mb, mg):
+                    finish_gate(s, mb, mg)
+            if x_pair:
+                x_quantise(x_pair)
+            for call in later.get(s, []):
+                call()

@@ -27,6 +27,7 @@ PAIRS = TILES // PAIR
 ROW_TILES = FEAT // P
 BLOCKS = PAIRS * N_GATES
 GROUPS = BLOCKS * PAIR
+WARM_UPS = 4
 MX_LEAD = 8
 
 FLOPS = 2 * BATCH * FEAT * GATE_COLS * 2
@@ -58,6 +59,7 @@ def tile_int8lstmcell_kernel(
         bias_rows = keep.tile([P, GATE_COLS], BF16)
         bias_all = keep.tile([P, GATE_COLS], F32)
         ones = keep.tile([P, P], BF16)
+        zeros = keep.tile([P, FEAT], BF16)
         ident_f32 = keep.tile([P, P], F32)
         warm = keep.tile([P, 1], F32)
         x_grouped = keep.tile([P, BATCH * 4], BF16, align_bytes=64)
@@ -71,12 +73,13 @@ def tile_int8lstmcell_kernel(
         c_new = keep.tile([P, TILES, FEAT], F32)
         h_new = keep.tile([P, TILES, FEAT], F32)
 
-        def gate(b, g):
-            return gates[:, b, g * FEAT : (g + 1) * FEAT]
+        def gate(b, g, lo=0, hi=FEAT):
+            return gates[:, b, g * FEAT + lo : g * FEAT + hi]
 
+        nc.vector.memset(ones[:], 1.0)
+        nc.gpsimd.memset(zeros[:], 0.0)
         nc.vector.memset(bias_rows[:].bitcast(I32), 0)
         nc.vector.memset(w_plane[:].bitcast(I32), 0)
-        nc.vector.memset(ones[:], 1.0)
         nc.vector.memset(warm[:], 0.0)
         make_identity(nc, ident_f32[:])
         nc.scalar.activation(out=warm[:], in_=warm[:], func=SIGMOID)
@@ -162,11 +165,12 @@ def tile_int8lstmcell_kernel(
 
         begun = set()
 
-        def fetch(sums_ps, b, g):
+        def fetch(sums_ps, b, g, lo=0, hi=FEAT):
             complete = (b, g) in begun
-            other = gate(b, g) if complete else bias_all[:, g * FEAT : (g + 1) * FEAT]
-            nc.vector.tensor_tensor(out=gate(b, g), in0=sums_ps[:], in1=other, op=ADD)
-            begun.add((b, g))
+            other = gate(b, g, lo, hi) if complete else bias_all[:, g * FEAT + lo : g * FEAT + hi]
+            nc.vector.tensor_tensor(out=gate(b, g, lo, hi), in0=sums_ps[:], in1=other, op=ADD)
+            if hi == FEAT:
+                begun.add((b, g))
             return complete
 
         def w_flip(jj):
@@ -185,11 +189,11 @@ def tile_int8lstmcell_kernel(
         def flip_copy(flip_ps, flip):
             nc.scalar.copy(out=flip[1], in_=flip_ps[:].rearrange("p j i r -> p j (i r)"))
 
-        def plain_matmuls(pl_ps, b, g, lo, hi, riders):
+        def plain_matmuls(sums, b, g, lo, hi, riders):
             share = -(-len(riders) // (K_CHUNKS - 1))
             for kc in range(K_CHUNKS):
                 nc.tensor.matmul(
-                    out=pl_ps[:, lo:hi],
+                    out=sums,
                     lhsT=h_t_halves[:, kc // 2, b * P : (b + 1) * P, kc % 2],
                     rhs=w_t_halves[:, kc // 2, g * FEAT + lo : g * FEAT + hi, kc % 2],
                     start=(kc == 0),
@@ -200,11 +204,11 @@ def tile_int8lstmcell_kernel(
 
         def plain_group(b, g, riders):
             pl_ps = psum.tile([P, FEAT], F32, tag="bank")
-            plain_matmuls(pl_ps, b, g, 0, FEAT, riders)
+            plain_matmuls(pl_ps[:], b, g, 0, FEAT, riders)
             return pl_ps
 
-        def activate(b, g):
-            nc.scalar.activation(out=gate(b, g), in_=gate(b, g), func=(TANH if g == 2 else SIGMOID))
+        def activate(b, g, lo=0, hi=FEAT):
+            nc.scalar.activation(out=gate(b, g, lo, hi), in_=gate(b, g, lo, hi), func=(TANH if g == 2 else SIGMOID))
 
         def f_times_c(cell, b):
             cell.tensor_tensor(out=gate(b, 1), in0=gate(b, 1), in1=c_sb[:, b, :], op=MULT)
@@ -219,9 +223,9 @@ def tile_int8lstmcell_kernel(
         def tanh_c_new(b):
             nc.scalar.activation(out=gate(b, 2), in_=c_new[:, b, :], func=TANH)
 
-        def h_product(cell, b):
-            cell.tensor_tensor(out=h_new[:, b, :], in0=gate(b, 3), in1=gate(b, 2), op=MULT)
-            nc.sync.dma_start(out=h_new_view[:, b, :], in_=h_new[:, b, :])
+        def h_product(cell, b, lo=0, hi=FEAT):
+            cell.tensor_tensor(out=h_new[:, b, lo:hi], in0=gate(b, 3, lo, hi), in1=gate(b, 2, lo, hi), op=MULT)
+            nc.sync.dma_start(out=h_new_view[:, b, lo:hi], in_=h_new[:, b, lo:hi])
 
         def flip_now(flip):
             flip_ps = psum.tile([P, WORD_CHUNKS, PAIR, P], F32, tag="bank")
@@ -235,6 +239,9 @@ def tile_int8lstmcell_kernel(
             nc.tensor.matmul(out=bias_ps[:], lhsT=ones[:], rhs=bias_rows[:, cols], start=True, stop=True)
             copy(out=bias_all[:, cols], in_=bias_ps[:])
 
+        warm_ps = psum.tile([P, FEAT], F32, tag="bank")
+        for i in range(WARM_UPS):
+            nc.tensor.matmul(out=warm_ps[:], lhsT=ones[:], rhs=zeros[:], start=True, stop=True)
         flip_now(h_flip(0))
         flip_now(w_flip(0))
         spread_biases(0, nc.vector.tensor_copy)
@@ -247,6 +254,10 @@ def tile_int8lstmcell_kernel(
                 block_order.append((q - 1, N_GATES - 1))
         block_order.append((PAIRS - 1, N_GATES - 1))
         groups = [(q * PAIR + t, g) for q, g in block_order for t in range(PAIR)]
+        first_of_last = groups.index(((PAIRS - 1) * PAIR, 0))
+        groups[first_of_last : first_of_last + PAIR * (N_GATES - 1)] = [
+            ((PAIRS - 1) * PAIR + t, g) for t in range(PAIR) for g in range(N_GATES - 1)
+        ]
 
         later = {}
 
@@ -258,7 +269,10 @@ def tile_int8lstmcell_kernel(
             last_pair = b // PAIR == PAIRS - 1
             last_tile = b == TILES - 1
             if g == 1:
-                f_times_c(nc.gpsimd, b)
+                if last_tile:
+                    at_slot(s + 1, lambda: f_times_c(nc.vector, b))
+                else:
+                    f_times_c(nc.gpsimd, b)
             elif g == 2:
                 if last_tile:
                     at_slot(s + 1, lambda: i_times_g(nc.vector, b))
@@ -267,10 +281,10 @@ def tile_int8lstmcell_kernel(
                 else:
                     i_times_g(nc.gpsimd, b)
                     c_sum(nc.gpsimd, b)
-                    at_slot(s + (2 if last_pair else 4), lambda: tanh_c_new(b))
+                    at_slot(s + (3 if last_pair else 4), lambda: tanh_c_new(b))
             elif g == 3:
                 if last_pair:
-                    at_slot(GROUPS - 1, lambda: h_product(nc.vector, b))
+                    at_slot(s + 1, lambda: h_product(nc.vector, b))
                 else:
                     h_product(nc.gpsimd, b)
 
@@ -278,15 +292,15 @@ def tile_int8lstmcell_kernel(
         pl_0 = psum.tile([P, FEAT], F32, tag="bank")
         pl_1 = psum.tile([P, FEAT], F32, tag="bank")
         f_ps_0 = psum.tile([P, WORD_CHUNKS, PAIR, P], F32, tag="bank")
-        plain_matmuls(pl_0, 0, 0, 0, half, flip_transposes(f_ps_0, w_flip(2)))
+        plain_matmuls(pl_0[:, :half], 0, 0, 0, half, flip_transposes(f_ps_0, w_flip(2)))
         flip_copy(f_ps_0, w_flip(2))
         x_ps = psum.tile([P, PAIR, 2, P], F32, tag="bank")
-        plain_matmuls(pl_1, 1, 0, 0, half, x_transposes(x_ps, 0))
+        plain_matmuls(pl_1[:, :half], 1, 0, 0, half, x_transposes(x_ps, 0))
         x_copy(x_ps, 0)
         f_ps_1 = psum.tile([P, WORD_CHUNKS, PAIR, P], F32, tag="bank")
-        plain_matmuls(pl_0, 0, 0, half, FEAT, flip_transposes(f_ps_1, w_flip(3)))
+        plain_matmuls(pl_0[:, half:], 0, 0, half, FEAT, flip_transposes(f_ps_1, w_flip(3)))
         flip_copy(f_ps_1, w_flip(3))
-        plain_matmuls(pl_1, 1, 0, half, FEAT, [])
+        plain_matmuls(pl_1[:, half:], 1, 0, half, FEAT, [])
         for g in range(1, N_GATES):
             spread_biases(g, nc.scalar.copy)
         x_quantise(0)
@@ -299,7 +313,7 @@ def tile_int8lstmcell_kernel(
                 finish_gate(1, mb, mg)
 
         for s, (b, g) in enumerate(groups):
-            if s < PAIR:
+            if s < PAIR or s == GROUPS - 1:
                 continue
             q, t = divmod(b, PAIR)
             if q == 0 and g == 1:
@@ -342,3 +356,16 @@ def tile_int8lstmcell_kernel(
                 x_quantise(x_pair)
             for call in later.get(s, []):
                 call()
+
+        b, g = groups[GROUPS - 1]
+        end_0 = psum.tile([P, half], F32, tag="bank")
+        end_1 = psum.tile([P, half], F32, tag="bank")
+        for end_ps, lo in ((end_0, 0), (end_1, half)):
+            plain_matmuls(end_ps[:], b, g, lo, lo + half, [])
+        for end_ps, lo in ((end_0, 0), (end_1, half)):
+            fetch(end_ps, b, g, lo, lo + half)
+            activate(b, g, lo, lo + half)
+        for call in later.get(GROUPS - 1, []):
+            call()
+        for lo in (0, half):
+            h_product(nc.vector, b, lo, lo + half)

@@ -223,9 +223,13 @@ def tile_int8lstmcell_kernel(
         def tanh_c_new(b):
             nc.scalar.activation(out=gate(b, 2), in_=c_new[:, b, :], func=TANH)
 
-        def h_product(cell, b, lo=0, hi=FEAT):
-            cell.tensor_tensor(out=h_new[:, b, lo:hi], in0=gate(b, 3, lo, hi), in1=gate(b, 2, lo, hi), op=MULT)
+        def h_store(b, lo=0, hi=FEAT):
             nc.sync.dma_start(out=h_new_view[:, b, lo:hi], in_=h_new[:, b, lo:hi])
+
+        def h_product(cell, b, lo=0, hi=FEAT, store_now=True):
+            cell.tensor_tensor(out=h_new[:, b, lo:hi], in0=gate(b, 3, lo, hi), in1=gate(b, 2, lo, hi), op=MULT)
+            if store_now:
+                h_store(b, lo, hi)
 
         def flip_now(flip):
             flip_ps = psum.tile([P, WORD_CHUNKS, PAIR, P], F32, tag="bank")
@@ -243,9 +247,11 @@ def tile_int8lstmcell_kernel(
         for i in range(WARM_UPS):
             nc.tensor.matmul(out=warm_ps[:], lhsT=ones[:], rhs=zeros[:], start=True, stop=True)
         flip_now(h_flip(0))
-        flip_now(w_flip(0))
         spread_biases(0, nc.vector.tensor_copy)
+        flip_now(w_flip(0))
+        spread_biases(1, nc.vector.tensor_copy)
         flip_now(w_flip(1))
+        spread_biases(2, nc.vector.tensor_copy)
 
         block_order = []
         for q in range(PAIRS):
@@ -285,6 +291,11 @@ def tile_int8lstmcell_kernel(
             elif g == 3:
                 if last_pair:
                     at_slot(s + 1, lambda: h_product(nc.vector, b))
+                    at_slot(s + 1, lambda: h_store(b - 1))
+                elif b // PAIR == PAIRS - 2:
+                    h_product(nc.gpsimd, b, store_now=False)
+                    if b % PAIR == 0:
+                        at_slot(s + 1, lambda: h_store(b))
                 else:
                     h_product(nc.gpsimd, b)
 
@@ -301,8 +312,7 @@ def tile_int8lstmcell_kernel(
         plain_matmuls(pl_0[:, half:], 0, 0, half, FEAT, flip_transposes(f_ps_1, w_flip(3)))
         flip_copy(f_ps_1, w_flip(3))
         plain_matmuls(pl_1[:, half:], 1, 0, half, FEAT, [])
-        for g in range(1, N_GATES):
-            spread_biases(g, nc.scalar.copy)
+        spread_biases(3, nc.scalar.copy)
         x_quantise(0)
         mx_done = 2 * PAIR
         fetch(pl_0, 0, 0)

@@ -296,6 +296,8 @@ def tile_int8lstmcell_kernel(
                     h_product(nc.gpsimd, b, store_now=False)
                     if b % PAIR == 0:
                         at_slot(s + 1, lambda: h_store(b))
+                elif b < 2 * PAIR:
+                    at_slot(s + 1, lambda: h_product(nc.vector, b))
                 else:
                     h_product(nc.gpsimd, b)
 

@@ -199,8 +199,10 @@ def tile_int8lstmcell_kernel(
                     start=(kc == 0),
                     stop=(kc == K_CHUNKS - 1),
                 )
-                for out, in_, identity in riders[kc * share : (kc + 1) * share]:
-                    nc.tensor.transpose(out, in_, identity)
+                if kc > 0 or len(riders) > 2 * share:
+                    first = (kc - 1 if len(riders) <= 2 * share else kc) * share
+                    for out, in_, identity in riders[first : first + share]:
+                        nc.tensor.transpose(out, in_, identity)
 
         def plain_group(b, g, riders):
             pl_ps = psum.tile([P, FEAT], F32, tag="bank")

from contextlib import ExitStack

import concourse.mybir as mybir
from concourse.masks import make_identity

BF16 = mybir.dt.bfloat16
F32 = mybir.dt.float32
I32 = mybir.dt.int32
U32 = mybir.dt.uint32
U8 = mybir.dt.uint8
FP8X4 = mybir.dt.float8_e4m3fn_x4
ADD = mybir.AluOpType.add
MULT = mybir.AluOpType.mult
SIGMOID = mybir.ActivationFunctionType.Sigmoid
TANH = mybir.ActivationFunctionType.Tanh

P = 128
BATCH = 1024
FEAT = 512
N_GATES = 4
GATE_COLS = N_GATES * FEAT
TILES = BATCH // P
K_CHUNKS = FEAT // P
WORD_CHUNKS = FEAT // 2 // P
PAIR = 2
PAIRS = TILES // PAIR
ROW_TILES = FEAT // P
BLOCKS = PAIRS * N_GATES
GROUPS = BLOCKS * PAIR
WARM_UPS = 4
MX_LEAD = 8

FLOPS = 2 * BATCH * FEAT * GATE_COLS * 2


def tile_int8lstmcell_kernel(
    tc, x, h_prev, c_prev, w_ih_words, w_ih_scales, w_hh, bias_ih, bias_hh, out_0, out_1
):
    nc = tc.nc
    with ExitStack() as stack:
        keep = stack.enter_context(tc.tile_pool(name="keep", bufs=1))
        psum = stack.enter_context(tc.psum_pool(name="psum", bufs=8))
        stack.enter_context(tc.manual_schedule())

        x_view = x.rearrange("(p b) k -> p b k", b=TILES)
        h_view = h_prev.rearrange("(p b) k -> p b k", b=TILES)
        c_view = c_prev.rearrange("(p b) k -> p b k", b=TILES)
        h_new_view = out_0.rearrange("(p b) n -> p b n", b=TILES)
        c_new_view = out_1.rearrange("(p b) n -> p b n", b=TILES)
        w_hh_view = w_hh.rearrange("(j p) k -> p j k", p=P)
        words_view = w_ih_words[0].rearrange("p n t -> p (n t)")

        x_sb = keep.tile([P, TILES, FEAT], BF16)
        h_sb = keep.tile([P, TILES, FEAT], BF16)
        c_sb = keep.tile([P, TILES, FEAT], BF16)
        w_sb = keep.tile([P, N_GATES * ROW_TILES, FEAT], BF16)
        w_words = keep.tile([P, GATE_COLS], U32, align_bytes=64)
        w_plane = keep.tile([P, GATE_COLS], U8, align_bytes=64)
        bias_rows = keep.tile([P, GATE_COLS], BF16)
        bias_all = keep.tile([P, GATE_COLS], F32)
        ones = keep.tile([P, P], BF16)
        zeros = keep.tile([P, FEAT], BF16)
        ident_f32 = keep.tile([P, P], F32)
        warm = keep.tile([P, 1], F32)
        x_grouped = keep.tile([P, BATCH * 4], BF16, align_bytes=64)
        x_codes = keep.tile([P, BATCH], U32, align_bytes=64)
        x_plane = keep.tile([P, BATCH], U8, align_bytes=64)
        h_t = keep.tile([P, WORD_CHUNKS, BATCH], F32)
        w_t = keep.tile([P, WORD_CHUNKS, GATE_COLS], F32)
        h_t_halves = h_t[:].rearrange("p j r -> p (j r)").bitcast(BF16).rearrange("p (j r e) -> p j r e", j=WORD_CHUNKS, e=2)
        w_t_halves = w_t[:].rearrange("p j r -> p (j r)").bitcast(BF16).rearrange("p (j r e) -> p j r e", j=WORD_CHUNKS, e=2)
        gates = keep.tile([P, TILES, GATE_COLS], F32)
        c_new = keep.tile([P, TILES, FEAT], F32)
        h_new = keep.tile([P, TILES, FEAT], F32)

        def gate(b, g, lo=0, hi=FEAT):
            return gates[:, b, g * FEAT + lo : g * FEAT + hi]

        nc.vector.memset(ones[:], 1.0)
        nc.gpsimd.memset(zeros[:], 0.0)
        nc.vector.memset(bias_rows[:].bitcast(I32), 0)
        nc.vector.memset(w_plane[:].bitcast(I32), 0)
        nc.vector.memset(warm[:], 0.0)
        make_identity(nc, ident_f32[:])
        nc.scalar.activation(out=warm[:], in_=warm[:], func=SIGMOID)

        def load_pair(dst, src, q):
            nc.sync.dma_start(out=dst[:, q * PAIR : (q + 1) * PAIR, :], in_=src[:, q * PAIR : (q + 1) * PAIR, :])

        def load_w_hh(jj):
            row_tiles = slice(jj * PAIR, (jj + 1) * PAIR)
            nc.sync.dma_start(out=w_sb[:, row_tiles, :], in_=w_hh_view[:, row_tiles, :])

        def load_words(g):
            nc.sync.dma_start(
                out=w_words[:, g * FEAT : (g + 1) * FEAT].bitcast(I32),
                in_=words_view[:, g * FEAT * 4 : (g + 1) * FEAT * 4].bitcast(I32),
            )

        load_pair(h_sb, h_view, 0)
        nc.sync.dma_start(out=bias_rows[0:1, :], in_=bias_ih.rearrange("(o n) -> o n", o=1))
        nc.sync.dma_start(out=bias_rows[1:2, :], in_=bias_hh.rearrange("(o n) -> o n", o=1))
        load_w_hh(0)
        load_w_hh(1)
        load_w_hh(2)
        load_pair(x_sb, x_view, 0)
        load_w_hh(3)
        for s in range(4):
            nc.sync.dma_start(
                out=w_plane[32 * s : 32 * s + 4, :].bitcast(I32),
                in_=w_ih_scales[0, 4 * s : 4 * s + 4, :].bitcast(I32),
            )
        load_words(0)
        load_words(1)
        load_w_hh(4)
        load_pair(x_sb, x_view, 1)
        load_w_hh(5)
        load_words(2)
        load_w_hh(6)
        load_w_hh(7)
        load_words(3)
        for q in range(PAIRS):
            load_pair(c_sb, c_view, q)
            if q + 1 < PAIRS:
                load_pair(h_sb, h_view, q + 1)
            if q + 2 < PAIRS:
                load_pair(x_sb, x_view, q + 2)

        grouped_words = x_grouped[:].bitcast(F32).rearrange("p (b r u) -> p b r u", b=TILES, u=2)

        def x_transposes(x_ps, q):
            return [
                (x_ps[:, t, u, :], x_sb[:, q * PAIR + t, :].bitcast(F32)[:, u : FEAT // 2 : 2], ident_f32[:])
                for t in range(PAIR)
                for u in range(2)
            ]

        def x_copy(x_ps, q):
            nc.scalar.copy(
                out=grouped_words[:, q * PAIR : (q + 1) * PAIR, :, :], in_=x_ps[:].rearrange("p t u r -> p t r u")
            )

        def x_quantise(q):
            rows = slice(q * PAIR * P, (q + 1) * PAIR * P)
            nc.vector.quantize_mx(
                out=x_codes[:, rows].bitcast(FP8X4),
                scales=x_plane[:, rows],
                in_=x_grouped[:, q * PAIR * P * 4 : (q + 1) * PAIR * P * 4],
            )

        def mx_pass(b, g):
            rows = slice(b * P, (b + 1) * P)
            cols = slice(g * FEAT, (g + 1) * FEAT)
            mx_ps = psum.tile([P, FEAT], F32, tag="bank")
            nc.tensor.matmul_mx(
                out=mx_ps[:],
                lhsT=x_codes[:, rows].bitcast(FP8X4),
                lhsT_scale=x_plane[:, rows],
                rhs=w_words[:, cols].bitcast(FP8X4),
                rhs_scale=w_plane[:, cols],
                start=True,
                stop=True,
            )
            return mx_ps

        begun = set()

        def fetch(sums_ps, b, g, lo=0, hi=FEAT):
            complete = (b, g) in begun
            other = gate(b, g, lo, hi) if complete else bias_all[:, g * FEAT + lo : g * FEAT + hi]
            nc.vector.tensor_tensor(out=gate(b, g, lo, hi), in0=sums_ps[:], in1=other, op=ADD)
            if hi == FEAT:
                begun.add((b, g))
            return complete

        def w_flip(jj):
            return ([w_sb[:, jj * PAIR + i, :] for i in range(PAIR)], w_t[:, :, jj * PAIR * P : (jj + 1) * PAIR * P])

        def h_flip(q):
            return ([h_sb[:, q * PAIR + i, :] for i in range(PAIR)], h_t[:, :, q * PAIR * P : (q + 1) * PAIR * P])

        def flip_transposes(flip_ps, flip):
            return [
                (flip_ps[:, j, i, :], flip[0][i].bitcast(F32)[:, j * P : (j + 1) * P], ident_f32[:])
                for i in range(PAIR)
                for j in range(WORD_CHUNKS)
            ]

        def flip_copy(flip_ps, flip):
            nc.scalar.copy(out=flip[1], in_=flip_ps[:].rearrange("p j i r -> p j (i r)"))

        def plain_matmuls(sums, b, g, lo, hi, riders):
            share = -(-len(riders) // (K_CHUNKS - 1))
            for kc in range(K_CHUNKS):
                nc.tensor.matmul(
                    out=sums,
                    lhsT=h_t_halves[:, kc // 2, b * P : (b + 1) * P, kc % 2],
                    rhs=w_t_halves[:, kc // 2, g * FEAT + lo : g * FEAT + hi, kc % 2],
                    start=(kc == 0),
                    stop=(kc == K_CHUNKS - 1),
                )
                if kc > 0 or len(riders) > 2 * share:
                    first = (kc - 1 if len(riders) <= 2 * share else kc) * share
                    for out, in_, identity in riders[first : first + share]:
                        nc.tensor.transpose(out, in_, identity)

        def plain_group(b, g, riders):
            pl_ps = psum.tile([P, FEAT], F32, tag="bank")
            plain_matmuls(pl_ps[:], b, g, 0, FEAT, riders)
            return pl_ps

        def activate(b, g, lo=0, hi=FEAT):
            nc.scalar.activation(out=gate(b, g, lo, hi), in_=gate(b, g, lo, hi), func=(TANH if g == 2 else SIGMOID))

        def f_times_c(cell, b):
            cell.tensor_tensor(out=gate(b, 1), in0=gate(b, 1), in1=c_sb[:, b, :], op=MULT)

        def i_times_g(cell, b):
            cell.tensor_tensor(out=gate(b, 0), in0=gate(b, 0), in1=gate(b, 2), op=MULT)

        def c_sum(cell, b):
            cell.tensor_tensor(out=c_new[:, b, :], in0=gate(b, 1), in1=gate(b, 0), op=ADD)
            nc.sync.dma_start(out=c_new_view[:, b, :], in_=c_new[:, b, :])

        def tanh_c_new(b):
            nc.scalar.activation(out=gate(b, 2), in_=c_new[:, b, :], func=TANH)

        def h_store(b, lo=0, hi=FEAT):
            nc.sync.dma_start(out=h_new_view[:, b, lo:hi], in_=h_new[:, b, lo:hi])

        def h_product(cell, b, lo=0, hi=FEAT, store_now=True):
            cell.tensor_tensor(out=h_new[:, b, lo:hi], in0=gate(b, 3, lo, hi), in1=gate(b, 2, lo, hi), op=MULT)
            if store_now:
                h_store(b, lo, hi)

        def flip_now(flip):
            flip_ps = psum.tile([P, WORD_CHUNKS, PAIR, P], F32, tag="bank")
            for out, in_, identity in flip_transposes(flip_ps, flip):
                nc.tensor.transpose(out, in_, identity)
            flip_copy(flip_ps, flip)

        def spread_biases(g, copy):
            cols = slice(g * FEAT, (g + 1) * FEAT)
            bias_ps = psum.tile([P, FEAT], F32, tag="bank")
            nc.tensor.matmul(out=bias_ps[:], lhsT=ones[:], rhs=bias_rows[:, cols], start=True, stop=True)
            copy(out=bias_all[:, cols], in_=bias_ps[:])

        warm_ps = psum.tile([P, FEAT], F32, tag="bank")
        for i in range(WARM_UPS):
            nc.tensor.matmul(out=warm_ps[:], lhsT=ones[:], rhs=zeros[:], start=True, stop=True)
        flip_now(h_flip(0))
        spread_biases(0, nc.vector.tensor_copy)
        flip_now(w_flip(0))
        spread_biases(1, nc.vector.tensor_copy)
        flip_now(w_flip(1))
        spread_biases(2, nc.vector.tensor_copy)

        block_order = []
        for q in range(PAIRS):
            block_order.extend([(q, g) for g in range(N_GATES - 1)])
            if q > 0:
                block_order.append((q - 1, N_GATES - 1))
        block_order.append((PAIRS - 1, N_GATES - 1))
        groups = [(q * PAIR + t, g) for q, g in block_order for t in range(PAIR)]
        first_of_last = groups.index(((PAIRS - 1) * PAIR, 0))
        groups[first_of_last : first_of_last + PAIR * (N_GATES - 1)] = [
            ((PAIRS - 1) * PAIR + t, g) for t in range(PAIR) for g in range(N_GATES - 1)
        ]

        later = {}

        def at_slot(s, call):
            later.setdefault(s, []).append(call)

        def finish_gate(s, b, g):
            activate(b, g)
            last_pair = b // PAIR == PAIRS - 1
            last_tile = b == TILES - 1
            if g == 1:
                if last_tile:
                    at_slot(s + 1, lambda: f_times_c(nc.vector, b))
                else:
                    f_times_c(nc.gpsimd, b)
            elif g == 2:
                if last_tile:
                    at_slot(s + 1, lambda: i_times_g(nc.vector, b))
                    at_slot(s + 2, lambda: c_sum(nc.vector, b))
                    at_slot(s + 2, lambda: tanh_c_new(b))
                else:
                    i_times_g(nc.gpsimd, b)
                    c_sum(nc.gpsimd, b)
                    at_slot(s + (3 if last_pair else 4), lambda: tanh_c_new(b))
            elif g == 3:
                if last_pair:
                    at_slot(s + 1, lambda: h_product(nc.vector, b))
                    at_slot(s + 1, lambda: h_store(b - 1))
                elif b // PAIR == PAIRS - 2:
                    h_product(nc.gpsimd, b, store_now=False)
                    if b % PAIR == 0:
                        at_slot(s + 1, lambda: h_store(b))
                elif b < 2 * PAIR:
                    at_slot(s + 1, lambda: h_product(nc.vector, b))
                else:
                    h_product(nc.gpsimd, b)

        half = FEAT // 2
        pl_0 = psum.tile([P, FEAT], F32, tag="bank")
        pl_1 = psum.tile([P, FEAT], F32, tag="bank")
        f_ps_0 = psum.tile([P, WORD_CHUNKS, PAIR, P], F32, tag="bank")
        plain_matmuls(pl_0[:, :half], 0, 0, 0, half, flip_transposes(f_ps_0, w_flip(2)))
        flip_copy(f_ps_0, w_flip(2))
        x_ps = psum.tile([P, PAIR, 2, P], F32, tag="bank")
        plain_matmuls(pl_1[:, :half], 1, 0, 0, half, x_transposes(x_ps, 0))
        x_copy(x_ps, 0)
        f_ps_1 = psum.tile([P, WORD_CHUNKS, PAIR, P], F32, tag="bank")
        plain_matmuls(pl_0[:, half:], 0, 0, half, FEAT, flip_transposes(f_ps_1, w_flip(3)))
        flip_copy(f_ps_1, w_flip(3))
        plain_matmuls(pl_1[:, half:], 1, 0, half, FEAT, [])
        spread_biases(3, nc.scalar.copy)
        x_quantise(0)
        mx_done = 2 * PAIR
        fetch(pl_0, 0, 0)
        fetch(pl_1, 1, 0)
        passes = [(mx_pass(mb, mg), mb, mg) for mb, mg in groups[:mx_done]]
        for mx_ps, mb, mg in passes:
            if fetch(mx_ps, mb, mg):
                finish_gate(1, mb, mg)

        for s, (b, g) in enumerate(groups):
            if s < PAIR or s == GROUPS - 1:
                continue
            q, t = divmod(b, PAIR)
            if q == 0 and g == 1:
                flips = [w_flip((g + 1) * (ROW_TILES // PAIR) + t)]
            elif q == 1 and g == 0:
                flips = [w_flip(3 * (ROW_TILES // PAIR) + t)]
            elif g == 2 and t == 0 and q + 1 < PAIRS:
                flips = [h_flip(q + 1)]
            else:
                flips = []
            if s == PAIR:
                x_pair = 1
            elif g == 2 and t == 1 and q + 2 < PAIRS:
                x_pair = q + 2
            else:
                x_pair = 0
            banks = []
            riders = []
            for flip in flips:
                flip_ps = psum.tile([P, WORD_CHUNKS, PAIR, P], F32, tag="bank")
                banks.append(flip_ps)
                riders.extend(flip_transposes(flip_ps, flip))
            if x_pair:
                x_ps = psum.tile([P, PAIR, 2, P], F32, tag="bank")
                riders.extend(x_transposes(x_ps, x_pair))
            pl_ps = plain_group(b, g, riders)
            for flip, flip_ps in zip(flips, banks):
                flip_copy(flip_ps, flip)
            if x_pair:
                x_copy(x_ps, x_pair)
            mx_wanted = min(GROUPS, s + 1 + min(s + 1, MX_LEAD))
            passes = [(mx_pass(mb, mg), mb, mg) for mb, mg in groups[mx_done:mx_wanted]]
            mx_done = mx_wanted
            if fetch(pl_ps, b, g):
                finish_gate(s, b, g)
            for mx_ps, mb, mg in passes:
                if fetch(mx_ps, mb, mg):
                    finish_gate(s, mb, mg)
            if x_pair:
                x_quantise(x_pair)
            for call in later.get(s, []):
                call()

        b, g = groups[GROUPS - 1]
        end_0 = psum.tile([P, half], F32, tag="bank")
        end_1 = psum.tile([P, half], F32, tag="bank")
        for end_ps, lo in ((end_0, 0), (end_1, half)):
            plain_matmuls(end_ps[:], b, g, lo, lo + half, [])
        for end_ps, lo in ((end_0, 0), (end_1, half)):
            fetch(end_ps, b, g, lo, lo + half)
            activate(b, g, lo, lo + half)
        for call in later.get(GROUPS - 1, []):
            call()
        for lo in (0, half):
            h_product(nc.vector, b, lo, lo + half)
